import numpy as np
import ml_dtypes


def mxq(x, axis, fmt="e4m3"):
    dtype, down = {"e4m3": (ml_dtypes.float8_e4m3fn, 7), "e5m2": (ml_dtypes.float8_e5m2, 14)}[fmt]
    v = np.moveaxis(np.asarray(x, np.float32).astype(ml_dtypes.bfloat16).astype(np.float64), axis, -1)
    blocks = v.reshape(v.shape[:-1] + (-1, 32))
    amax = np.abs(blocks).max(-1, keepdims=True)
    byte = np.maximum(np.where(amax > 0, np.frexp(amax)[1] - 1 + 127, 0) - down, 1)
    scale = np.exp2(byte - 127.0)
    codes = (blocks / scale).astype(np.float32).astype(dtype).astype(np.float64)
    return np.moveaxis((codes * scale).reshape(v.shape), -1, axis)


WIDE = False


def mx_kscale(k):
    if not WIDE:
        return np.ones(k)
    levels = np.array([20, -20, 10, -10, 0])
    a = np.random.permutation(np.resize(levels, k // 512 * 4)).reshape(k // 512, 4)
    idx = np.arange(k)
    return np.exp2(a[idx // 512, idx % 128 // 32])


BF16 = ml_dtypes.bfloat16


def bf(x):
    return np.asarray(x, np.float32).astype(BF16)


def f64(x):
    return np.asarray(x).astype(np.float64)


B, IN_F, OUT_F, N_ACT = 2048, 1024, 512, 4


def sigmoid(v):
    return 1.0 / (1.0 + np.exp(-v))


def _cyclic_act_derivs(y):
    Bb, O = y.shape
    yg = y.reshape(Bb, O // N_ACT, N_ACT)
    th = np.tanh(yg[..., 0])
    sg = sigmoid(yg[..., 3])
    d = np.stack([
        1.0 - th * th,
        np.cos(yg[..., 1]),
        np.where(yg[..., 2] > 0.0, 1.0, 0.0),
        sg * (1.0 - sg),
    ], axis=-1)
    return d.reshape(Bb, O)


def setup_inputs():
    u = mx_kscale(OUT_F)
    limit = np.sqrt(6.0 / (IN_F + OUT_F))
    x = bf(np.random.standard_normal((B, IN_F)))
    W0 = bf(np.random.uniform(-limit, limit, (OUT_F, IN_F)))
    b = bf(np.random.standard_normal(OUT_F) * 0.1)
    g = bf(np.random.standard_normal((B, OUT_F)) * np.exp2(np.random.randint(-12, 1, (B, 1))) * 8.0 * u[None, :])
    y = f64(x) @ f64(W0).T + f64(b)
    return {"input": x, "W": bf(f64(W0) / u[:, None]), "b": b,
            "y": np.asarray(y, np.float32), "grad_out": g}


def reference(input, W, b, y, grad_out):
    dy = f64(grad_out) * _cyclic_act_derivs(f64(y))
    return mxq(dy, 1, "e5m2") @ mxq(f64(W), 0, "e4m3")

@@ -1,0 +1,189 @@
+from contextlib import ExitStack
+import math
+
+import concourse.mybir as mybir
+from concourse.masks import make_identity
+
+F32 = mybir.dt.float32
+BF16 = mybir.dt.bfloat16
+U32 = mybir.dt.uint32
+U8 = mybir.dt.uint8
+E5M2X4 = mybir.dt.float8_e5m2_x4
+E4M3X4 = mybir.dt.float8_e4m3fn_x4
+ACT = mybir.ActivationFunctionType
+ALU = mybir.AluOpType
+
+P = 128
+PACK = 4
+TOKENS = 2048
+OUT_F = 512
+IN_F = 1024
+WORDS = OUT_F // PACK
+N_HALF = 512
+HALVES = IN_F // N_HALF
+TOK_PER_PART = TOKENS // P
+T = 2
+GROUPS = TOK_PER_PART // T
+
+ROUND_MAGIC = 12582912.0
+
+FLOPS = 2 * TOKENS * OUT_F * IN_F
+BYTES = TOKENS * OUT_F * 4 + TOKENS * OUT_F * 2 + OUT_F * IN_F * 2 + TOKENS * IN_F * 4
+
+
+def tile_vdl_t_v_kernel(tc, x_in, w, b, y, grad_out, out):
+    nc = tc.nc
+    y_view = y.rearrange("(q i) k -> q i k", i=TOK_PER_PART)
+    g_view = grad_out.rearrange("(q i) k -> q i k", i=TOK_PER_PART)
+    out_view = out.rearrange("(q i) n -> q i n", i=TOK_PER_PART)
+
+    with ExitStack() as ctx:
+        consts = ctx.enter_context(tc.tile_pool(name="consts", bufs=1))
+        loads = ctx.enter_context(tc.tile_pool(name="loads", bufs=1))
+        work = ctx.enter_context(tc.tile_pool(name="work", bufs=3))
+        mx = ctx.enter_context(tc.tile_pool(name="mx", bufs=4))
+        outs = ctx.enter_context(tc.tile_pool(name="outs", bufs=8))
+        psum_t = ctx.enter_context(tc.psum_pool(name="psum_t", bufs=2))
+        psum_o = ctx.enter_context(tc.psum_pool(name="psum_o", bufs=6))
+
+        y_sb = []
+        g_sb = []
+        w_raw = loads.tile([P, PACK, IN_F], BF16, name="w_raw")
+        for grp in range(GROUPS):
+            rows = slice(grp * T, (grp + 1) * T)
+            y_t = loads.tile([P, T, OUT_F], F32, name="y%d" % grp)
+            nc.sync.dma_start(out=y_t[:], in_=y_view[:, rows, :])
+            g_t = loads.tile([P, T, OUT_F], BF16, name="g%d" % grp)
+            nc.sync.dma_start(out=g_t[:], in_=g_view[:, rows, :])
+            y_sb.append(y_t)
+            g_sb.append(g_t)
+            if grp == 1:
+                nc.sync.dma_start(out=w_raw[:], in_=w.rearrange("(p j) n -> p j n", j=PACK))
+
+        warm_in = consts.tile([P, 1], F32, name="warm_in")
+        warm_out = consts.tile([P, 1], F32, name="warm_out")
+        nc.vector.memset(warm_in[:], 0.0)
+        nc.scalar.activation(out=warm_out[:], in_=warm_in[:], func=ACT.Silu)
+
+        ident = consts.tile([P, P], BF16, name="ident")
+        make_identity(nc, ident[:])
+
+        w_grouped = consts.tile([P, IN_F, PACK], BF16, name="w_grouped", align_bytes=64)
+        w_codes = consts.tile([P, IN_F], U32, name="w_codes", align_bytes=64)
+        w_scales = consts.tile([P, IN_F], U8, name="w_scales", align_bytes=64)
+
+        def quantise_w(h):
+            cols = slice(h * N_HALF, (h + 1) * N_HALF)
+            nc.vector.tensor_copy(
+                out=w_grouped[:, cols, :].rearrange("p (c i) t -> p c t i", i=4),
+                in_=w_raw[:, :, cols].rearrange("p t (c i) -> p c t i", i=4),
+            )
+            nc.vector.quantize_mx(
+                out=w_codes[:, cols].bitcast(E4M3X4),
+                scales=w_scales[:, cols],
+                in_=w_grouped[:, cols, :].rearrange("p n t -> p (n t)"),
+            )
+
+        dy_of = {}
+        codes_of = {}
+
+        def gradient_of_preactivation(grp):
+            y4 = y_sb[grp][:].rearrange("p i (j c) -> p i j c", c=PACK)
+            g4 = g_sb[grp][:].rearrange("p i (j c) -> p i j c", c=PACK)
+            dy = work.tile([P, T, PACK, WORDS], BF16, name="dy")
+            dy_of[grp] = dy
+
+            turns = work.tile([P, T, WORDS], F32, name="turns")
+            whole = work.tile([P, T, WORDS], F32, name="whole")
+            frac = work.tile([P, T, WORDS], F32, name="frac")
+            nc.vector.tensor_scalar(
+                out=turns[:], in0=y4[:, :, :, 1], scalar1=1.0 / (2.0 * math.pi), scalar2=0.25,
+                op0=ALU.mult, op1=ALU.add,
+            )
+            nc.vector.tensor_scalar(
+                out=whole[:], in0=turns[:], scalar1=ROUND_MAGIC, scalar2=ROUND_MAGIC,
+                op0=ALU.add, op1=ALU.subtract,
+            )
+            nc.vector.tensor_tensor(out=frac[:], in0=turns[:], in1=whole[:], op=ALU.subtract)
+
+            th0 = work.tile([P, T, WORDS], F32, name="th0")
+            nsq0 = work.tile([P, T, WORDS], F32, name="nsq0")
+            th3 = work.tile([P, T, WORDS], F32, name="th3")
+            nsq3 = work.tile([P, T, WORDS], F32, name="nsq3")
+            cosy = work.tile([P, T, WORDS], F32, name="cosy")
+            nc.scalar.activation(out=th0[:], in_=y4[:, :, :, 0], func=ACT.Tanh)
+            nc.scalar.activation(out=th3[:], in_=y4[:, :, :, 3], func=ACT.Tanh, scale=0.5)
+            nc.scalar.activation(out=cosy[:], in_=frac[:], func=ACT.Sin, scale=2.0 * math.pi)
+
+            nc.vector.scalar_tensor_tensor(
+                out=dy[:, :, 2, :], in0=y4[:, :, :, 2], scalar=0.0, in1=g4[:, :, :, 2],
+                op0=ALU.is_gt, op1=ALU.mult,
+            )
+            nc.vector.scalar_tensor_tensor(
+                out=nsq0[:], in0=th0[:], scalar=-1.0, in1=th0[:], op0=ALU.mult, op1=ALU.mult
+            )
+            nc.vector.scalar_tensor_tensor(
+                out=dy[:, :, 0, :], in0=nsq0[:], scalar=1.0, in1=g4[:, :, :, 0],
+                op0=ALU.add, op1=ALU.mult,
+            )
+            nc.vector.scalar_tensor_tensor(
+                out=nsq3[:], in0=th3[:], scalar=-0.25, in1=th3[:], op0=ALU.mult, op1=ALU.mult
+            )
+            nc.vector.scalar_tensor_tensor(
+                out=dy[:, :, 3, :], in0=nsq3[:], scalar=0.25, in1=g4[:, :, :, 3],
+                op0=ALU.add, op1=ALU.mult,
+            )
+            nc.vector.tensor_tensor(
+                out=dy[:, :, 1, :], in0=cosy[:], in1=g4[:, :, :, 1], op=ALU.mult
+            )
+
+        def transpose_and_quantise(grp):
+            dy = dy_of[grp]
+            dy_t = psum_t.tile([P, T, PACK, P], BF16, name="dy_t")
+            for i in range(T):
+                for c in range(PACK):
+                    nc.tensor.transpose(dy_t[:, i, c, :], dy[:, i, c, :], ident[:])
+            grouped = work.tile([P, T, P, PACK], BF16, name="grouped", align_bytes=64)
+            nc.scalar.copy(out=grouped[:], in_=dy_t[:].rearrange("p i c t -> p i t c"))
+            codes = mx.tile([P, T * P], U32, name="codes", align_bytes=64)
+            scales = mx.tile([P, T * P], U8, name="scales", align_bytes=64)
+            nc.vector.quantize_mx(
+                out=codes[:].bitcast(E5M2X4),
+                scales=scales[:],
+                in_=grouped[:].rearrange("p i t c -> p (i t c)"),
+            )
+            codes_of[grp] = (codes, scales)
+
+        def multiply_and_store(grp):
+            codes, scales = codes_of[grp]
+            for i in range(T):
+                toks = slice(i * P, (i + 1) * P)
+                result = outs.tile([P, IN_F], F32, name="result")
+                for h in range(HALVES):
+                    cols = slice(h * N_HALF, (h + 1) * N_HALF)
+                    acc = psum_o.tile([P, N_HALF], F32, name="acc")
+                    nc.tensor.matmul_mx(
+                        out=acc[:],
+                        lhsT=codes[:, toks].bitcast(E5M2X4),
+                        lhsT_scale=scales[:, toks],
+                        rhs=w_codes[:, cols].bitcast(E4M3X4),
+                        rhs_scale=w_scales[:, cols],
+                        start=True,
+                        stop=True,
+                    )
+                    if i == T - 1 and h == HALVES - 1:
+                        nc.vector.tensor_copy(out=result[:, cols], in_=acc[:])
+                    else:
+                        nc.scalar.copy(out=result[:, cols], in_=acc[:])
+                nc.sync.dma_start(out=out_view[:, grp * T + i, :], in_=result[:])
+
+        for step in range(GROUPS + 2):
+            if step < GROUPS:
+                gradient_of_preactivation(step)
+            if step == 1:
+                for h in range(HALVES):
+                    quantise_w(h)
+            if step >= 2:
+                multiply_and_store(step - 2)
+            if 1 <= step <= GROUPS:
+                transpose_and_quantise(step - 1)

@@ -93,41 +93,40 @@ def tile_vdl_t_v_kernel(tc, x_in, w, b, y, grad_out, out):
             dy = work.tile([P, T, PACK, WORDS], BF16, name="dy")
             dy_of[grp] = dy
 
+            th0 = work.tile([P, T, WORDS], F32, name="th0")
+            th3 = work.tile([P, T, WORDS], F32, name="th3")
+            nc.scalar.activation(out=th0[:], in_=y4[:, :, :, 0], func=ACT.Tanh)
+            nc.scalar.activation(out=th3[:], in_=y4[:, :, :, 3], func=ACT.Tanh, scale=0.5)
+
             turns = work.tile([P, T, WORDS], F32, name="turns")
             whole = work.tile([P, T, WORDS], F32, name="whole")
             frac = work.tile([P, T, WORDS], F32, name="frac")
+            nsq0 = work.tile([P, T, WORDS], F32, name="nsq0")
+            nsq3 = work.tile([P, T, WORDS], F32, name="nsq3")
+            cosy = work.tile([P, T, WORDS], F32, name="cosy")
             nc.vector.tensor_scalar(
                 out=turns[:], in0=y4[:, :, :, 1], scalar1=1.0 / (2.0 * math.pi), scalar2=0.25,
                 op0=ALU.mult, op1=ALU.add,
+            )
+            nc.vector.scalar_tensor_tensor(
+                out=dy[:, :, 2, :], in0=y4[:, :, :, 2], scalar=0.0, in1=g4[:, :, :, 2],
+                op0=ALU.is_gt, op1=ALU.mult,
             )
             nc.vector.tensor_scalar(
                 out=whole[:], in0=turns[:], scalar1=ROUND_MAGIC, scalar2=ROUND_MAGIC,
                 op0=ALU.add, op1=ALU.subtract,
             )
-            nc.vector.tensor_tensor(out=frac[:], in0=turns[:], in1=whole[:], op=ALU.subtract)
-
-            th0 = work.tile([P, T, WORDS], F32, name="th0")
-            nsq0 = work.tile([P, T, WORDS], F32, name="nsq0")
-            th3 = work.tile([P, T, WORDS], F32, name="th3")
-            nsq3 = work.tile([P, T, WORDS], F32, name="nsq3")
-            cosy = work.tile([P, T, WORDS], F32, name="cosy")
-            nc.scalar.activation(out=th0[:], in_=y4[:, :, :, 0], func=ACT.Tanh)
-            nc.scalar.activation(out=th3[:], in_=y4[:, :, :, 3], func=ACT.Tanh, scale=0.5)
-            nc.scalar.activation(out=cosy[:], in_=frac[:], func=ACT.Sin, scale=2.0 * math.pi)
-
-            nc.vector.scalar_tensor_tensor(
-                out=dy[:, :, 2, :], in0=y4[:, :, :, 2], scalar=0.0, in1=g4[:, :, :, 2],
-                op0=ALU.is_gt, op1=ALU.mult,
-            )
             nc.vector.scalar_tensor_tensor(
                 out=nsq0[:], in0=th0[:], scalar=-1.0, in1=th0[:], op0=ALU.mult, op1=ALU.mult
             )
+            nc.vector.tensor_tensor(out=frac[:], in0=turns[:], in1=whole[:], op=ALU.subtract)
+            nc.vector.scalar_tensor_tensor(
+                out=nsq3[:], in0=th3[:], scalar=-0.25, in1=th3[:], op0=ALU.mult, op1=ALU.mult
+            )
+            nc.scalar.activation(out=cosy[:], in_=frac[:], func=ACT.Sin, scale=2.0 * math.pi)
             nc.vector.scalar_tensor_tensor(
                 out=dy[:, :, 0, :], in0=nsq0[:], scalar=1.0, in1=g4[:, :, :, 0],
                 op0=ALU.add, op1=ALU.mult,
-            )
-            nc.vector.scalar_tensor_tensor(
-                out=nsq3[:], in0=th3[:], scalar=-0.25, in1=th3[:], op0=ALU.mult, op1=ALU.mult
             )
             nc.vector.scalar_tensor_tensor(
                 out=dy[:, :, 3, :], in0=nsq3[:], scalar=0.25, in1=g4[:, :, :, 3],

@@ -25,6 +25,10 @@ TOK_PER_PART = TOKENS // P
 T = 2
 GROUPS = TOK_PER_PART // T
 
+VECTOR_ONE_FROM = 1
+VECTOR_TWO_FROM = 4
+W_AFTER = 2
+
 ROUND_MAGIC = 12582912.0
 
 FLOPS = 2 * TOKENS * OUT_F * IN_F
@@ -57,7 +61,7 @@ def tile_vdl_t_v_kernel(tc, x_in, w, b, y, grad_out, out):
             nc.sync.dma_start(out=g_t[:], in_=g_view[:, rows, :])
             y_sb.append(y_t)
             g_sb.append(g_t)
-            if grp == 1:
+            if grp == W_AFTER:
                 nc.sync.dma_start(out=w_raw[:], in_=w.rearrange("(p j) n -> p j n", j=PACK))
 
         warm_in = consts.tile([P, 1], F32, name="warm_in")
@@ -72,95 +76,112 @@ def tile_vdl_t_v_kernel(tc, x_in, w, b, y, grad_out, out):
         w_codes = consts.tile([P, IN_F], U32, name="w_codes", align_bytes=64)
         w_scales = consts.tile([P, IN_F], U8, name="w_scales", align_bytes=64)
 
-        def quantise_w(h):
-            cols = slice(h * N_HALF, (h + 1) * N_HALF)
-            nc.vector.tensor_copy(
-                out=w_grouped[:, cols, :].rearrange("p (c i) t -> p c t i", i=4),
-                in_=w_raw[:, :, cols].rearrange("p t (c i) -> p c t i", i=4),
-            )
-            nc.vector.quantize_mx(
-                out=w_codes[:, cols].bitcast(E4M3X4),
-                scales=w_scales[:, cols],
-                in_=w_grouped[:, cols, :].rearrange("p n t -> p (n t)"),
-            )
+        def halves():
+            return [slice(h * N_HALF, (h + 1) * N_HALF) for h in range(HALVES)]
 
-        dy_of = {}
-        codes_of = {}
+        def prepare_w():
+            for cols in halves():
+                nc.vector.tensor_copy(
+                    out=w_grouped[:, cols, :].rearrange("p (c i) t -> p c t i", i=4),
+                    in_=w_raw[:, :, cols].rearrange("p t (c i) -> p c t i", i=4),
+                )
+            for cols in halves():
+                nc.vector.quantize_mx(
+                    out=w_codes[:, cols].bitcast(E4M3X4),
+                    scales=w_scales[:, cols],
+                    in_=w_grouped[:, cols, :].rearrange("p n t -> p (n t)"),
+                )
 
-        def gradient_of_preactivation(grp):
-            y4 = y_sb[grp][:].rearrange("p i (j c) -> p i j c", c=PACK)
-            g4 = g_sb[grp][:].rearrange("p i (j c) -> p i j c", c=PACK)
-            dy = work.tile([P, T, PACK, WORDS], BF16, name="dy")
-            dy_of[grp] = dy
+        kept = {}
 
-            th0 = work.tile([P, T, WORDS], F32, name="th0")
-            th3 = work.tile([P, T, WORDS], F32, name="th3")
-            nc.scalar.activation(out=th0[:], in_=y4[:, :, :, 0], func=ACT.Tanh)
-            nc.scalar.activation(out=th3[:], in_=y4[:, :, :, 3], func=ACT.Tanh, scale=0.5)
+        def columns(tiles, grp):
+            return tiles[grp][:].rearrange("p i (j c) -> p i j c", c=PACK)
 
-            turns = work.tile([P, T, WORDS], F32, name="turns")
-            whole = work.tile([P, T, WORDS], F32, name="whole")
-            frac = work.tile([P, T, WORDS], F32, name="frac")
-            nsq0 = work.tile([P, T, WORDS], F32, name="nsq0")
-            nsq3 = work.tile([P, T, WORDS], F32, name="nsq3")
-            cosy = work.tile([P, T, WORDS], F32, name="cosy")
+        def new(name, grp, dtype=F32, shape=(P, T, WORDS)):
+            kept[name, grp] = work.tile(list(shape), dtype, name=name)
+            return kept[name, grp]
+
+        def turns_of(grp):
             nc.vector.tensor_scalar(
-                out=turns[:], in0=y4[:, :, :, 1], scalar1=1.0 / (2.0 * math.pi), scalar2=0.25,
-                op0=ALU.mult, op1=ALU.add,
+                out=new("turns", grp)[:], in0=columns(y_sb, grp)[:, :, :, 1],
+                scalar1=1.0 / (2.0 * math.pi), scalar2=0.25, op0=ALU.mult, op1=ALU.add,
             )
-            nc.vector.scalar_tensor_tensor(
-                out=dy[:, :, 2, :], in0=y4[:, :, :, 2], scalar=0.0, in1=g4[:, :, :, 2],
-                op0=ALU.is_gt, op1=ALU.mult,
-            )
+
+        def whole_of(grp):
             nc.vector.tensor_scalar(
-                out=whole[:], in0=turns[:], scalar1=ROUND_MAGIC, scalar2=ROUND_MAGIC,
-                op0=ALU.add, op1=ALU.subtract,
+                out=new("whole", grp)[:], in0=kept["turns", grp][:], scalar1=ROUND_MAGIC,
+                scalar2=ROUND_MAGIC, op0=ALU.add, op1=ALU.subtract,
             )
-            nc.vector.scalar_tensor_tensor(
-                out=nsq0[:], in0=th0[:], scalar=-1.0, in1=th0[:], op0=ALU.mult, op1=ALU.mult
-            )
-            nc.vector.tensor_tensor(out=frac[:], in0=turns[:], in1=whole[:], op=ALU.subtract)
-            nc.vector.scalar_tensor_tensor(
-                out=nsq3[:], in0=th3[:], scalar=-0.25, in1=th3[:], op0=ALU.mult, op1=ALU.mult
-            )
-            nc.scalar.activation(out=cosy[:], in_=frac[:], func=ACT.Sin, scale=2.0 * math.pi)
-            nc.vector.scalar_tensor_tensor(
-                out=dy[:, :, 0, :], in0=nsq0[:], scalar=1.0, in1=g4[:, :, :, 0],
-                op0=ALU.add, op1=ALU.mult,
-            )
-            nc.vector.scalar_tensor_tensor(
-                out=dy[:, :, 3, :], in0=nsq3[:], scalar=0.25, in1=g4[:, :, :, 3],
-                op0=ALU.add, op1=ALU.mult,
-            )
+
+        def frac_of(grp):
             nc.vector.tensor_tensor(
-                out=dy[:, :, 1, :], in0=cosy[:], in1=g4[:, :, :, 1], op=ALU.mult
+                out=new("frac", grp)[:], in0=kept["turns", grp][:], in1=kept["whole", grp][:],
+                op=ALU.subtract,
             )
 
-        def transpose_and_quantise(grp):
-            dy = dy_of[grp]
+        def functions_of(grp):
+            y4 = columns(y_sb, grp)
+            nc.scalar.activation(out=new("th0", grp)[:], in_=y4[:, :, :, 0], func=ACT.Tanh)
+            nc.scalar.activation(out=new("th3", grp)[:], in_=y4[:, :, :, 3], func=ACT.Tanh, scale=0.5)
+            nc.scalar.activation(
+                out=new("cosy", grp)[:], in_=kept["frac", grp][:], func=ACT.Sin, scale=2.0 * math.pi
+            )
+
+        def relu_column(grp):
+            dy = new("dy", grp, BF16, (P, T, PACK, WORDS))
+            nc.vector.scalar_tensor_tensor(
+                out=dy[:, :, 2, :], in0=columns(y_sb, grp)[:, :, :, 2], scalar=0.0,
+                in1=columns(g_sb, grp)[:, :, :, 2], op0=ALU.is_gt, op1=ALU.mult,
+            )
+
+        def minus_square(grp, name, source, factor):
+            th = kept[source, grp]
+            nc.vector.scalar_tensor_tensor(
+                out=new(name, grp)[:], in0=th[:], scalar=-factor, in1=th[:], op0=ALU.mult, op1=ALU.mult
+            )
+
+        def squared_column(grp, c, name, factor):
+            nc.vector.scalar_tensor_tensor(
+                out=kept["dy", grp][:, :, c, :], in0=kept[name, grp][:], scalar=factor,
+                in1=columns(g_sb, grp)[:, :, :, c], op0=ALU.add, op1=ALU.mult,
+            )
+
+        def cos_column(grp):
+            nc.vector.tensor_tensor(
+                out=kept["dy", grp][:, :, 1, :], in0=kept["cosy", grp][:],
+                in1=columns(g_sb, grp)[:, :, :, 1], op=ALU.mult,
+            )
+
+        def transposes(grp):
+            dy = kept["dy", grp]
             dy_t = psum_t.tile([P, T, PACK, P], BF16, name="dy_t")
+            kept["dy_t", grp] = dy_t
             for i in range(T):
                 for c in range(PACK):
                     nc.tensor.transpose(dy_t[:, i, c, :], dy[:, i, c, :], ident[:])
+
+        def interleave(grp):
             grouped = work.tile([P, T, P, PACK], BF16, name="grouped", align_bytes=64)
-            nc.scalar.copy(out=grouped[:], in_=dy_t[:].rearrange("p i c t -> p i t c"))
+            kept["grouped", grp] = grouped
+            nc.scalar.copy(out=grouped[:], in_=kept["dy_t", grp][:].rearrange("p i c t -> p i t c"))
+
+        def quantise(grp):
             codes = mx.tile([P, T * P], U32, name="codes", align_bytes=64)
             scales = mx.tile([P, T * P], U8, name="scales", align_bytes=64)
             nc.vector.quantize_mx(
                 out=codes[:].bitcast(E5M2X4),
                 scales=scales[:],
-                in_=grouped[:].rearrange("p i t c -> p (i t c)"),
+                in_=kept["grouped", grp][:].rearrange("p i t c -> p (i t c)"),
             )
-            codes_of[grp] = (codes, scales)
+            kept["codes", grp] = (codes, scales)
 
-        def multiply_and_store(grp):
-            codes, scales = codes_of[grp]
+        def multiply(grp):
+            codes, scales = kept["codes", grp]
             for i in range(T):
                 toks = slice(i * P, (i + 1) * P)
-                result = outs.tile([P, IN_F], F32, name="result")
-                for h in range(HALVES):
-                    cols = slice(h * N_HALF, (h + 1) * N_HALF)
+                for h, cols in enumerate(halves()):
                     acc = psum_o.tile([P, N_HALF], F32, name="acc")
+                    kept["acc", grp, i, h] = acc
                     nc.tensor.matmul_mx(
                         out=acc[:],
                         lhsT=codes[:, toks].bitcast(E5M2X4),
@@ -170,19 +191,52 @@ def tile_vdl_t_v_kernel(tc, x_in, w, b, y, grad_out, out):
                         start=True,
                         stop=True,
                     )
-                    if i == T - 1 and h == HALVES - 1:
+
+        def empty_and_store(grp):
+            for i in range(T):
+                result = outs.tile([P, IN_F], F32, name="result")
+                for h, cols in enumerate(halves()):
+                    acc = kept["acc", grp, i, h]
+                    if h == 0 and grp >= (VECTOR_ONE_FROM if i == 0 else VECTOR_TWO_FROM):
                         nc.vector.tensor_copy(out=result[:, cols], in_=acc[:])
                     else:
                         nc.scalar.copy(out=result[:, cols], in_=acc[:])
                 nc.sync.dma_start(out=out_view[:, grp * T + i, :], in_=result[:])
 
-        for step in range(GROUPS + 2):
-            if step < GROUPS:
-                gradient_of_preactivation(step)
-            if step == 1:
-                for h in range(HALVES):
-                    quantise_w(h)
-            if step >= 2:
-                multiply_and_store(step - 2)
-            if 1 <= step <= GROUPS:
-                transpose_and_quantise(step - 1)
+        def is_group(grp):
+            return 0 <= grp < GROUPS
+
+        with tc.manual_schedule():
+            turns_of(0)
+            whole_of(0)
+            frac_of(0)
+            functions_of(0)
+            for r in range(GROUPS + 2):
+                if r == W_AFTER:
+                    prepare_w()
+                if is_group(r - 2):
+                    quantise(r - 2)
+                    multiply(r - 2)
+                if is_group(r - 1):
+                    interleave(r - 1)
+                ahead = is_group(r + 1)
+                if is_group(r):
+                    relu_column(r)
+                if ahead:
+                    turns_of(r + 1)
+                if is_group(r):
+                    minus_square(r, "nsq0", "th0", 1.0)
+                if ahead:
+                    whole_of(r + 1)
+                if is_group(r):
+                    minus_square(r, "nsq3", "th3", 0.25)
+                if ahead:
+                    frac_of(r + 1)
+                    functions_of(r + 1)
+                if is_group(r):
+                    squared_column(r, 0, "nsq0", 1.0)
+                    squared_column(r, 3, "nsq3", 0.25)
+                    cos_column(r)
+                    transposes(r)
+                if is_group(r - 2):
+                    empty_and_store(r - 2)

@@ -22,11 +22,11 @@ WORDS = OUT_F // PACK
 N_HALF = 512
 HALVES = IN_F // N_HALF
 TOK_PER_PART = TOKENS // P
-T = 2
-GROUPS = TOK_PER_PART // T
+SIZES = (2, 2, 2, 2, 2, 2, 2, 1, 1)
+GROUPS = len(SIZES)
 
-VECTOR_ONE_FROM = 1
-VECTOR_TWO_FROM = 4
+VECTOR_EVEN_FROM = 2
+VECTOR_ODD_FROM = 5
 W_AFTER = 2
 
 ROUND_MAGIC = 12582912.0
@@ -37,6 +37,7 @@ BYTES = TOKENS * OUT_F * 4 + TOKENS * OUT_F * 2 + OUT_F * IN_F * 2 + TOKENS * IN
 
 def tile_vdl_t_v_kernel(tc, x_in, w, b, y, grad_out, out):
     nc = tc.nc
+    FIRST = [sum(SIZES[:grp]) for grp in range(GROUPS)]
     y_view = y.rearrange("(q i) k -> q i k", i=TOK_PER_PART)
     g_view = grad_out.rearrange("(q i) k -> q i k", i=TOK_PER_PART)
     out_view = out.rearrange("(q i) n -> q i n", i=TOK_PER_PART)
@@ -53,8 +54,8 @@ def tile_vdl_t_v_kernel(tc, x_in, w, b, y, grad_out, out):
         y_sb = []
         g_sb = []
         w_raw = loads.tile([P, PACK, IN_F], BF16, name="w_raw")
-        for grp in range(GROUPS):
-            rows = slice(grp * T, (grp + 1) * T)
+        for grp, T in enumerate(SIZES):
+            rows = slice(FIRST[grp], FIRST[grp] + T)
             y_t = loads.tile([P, T, OUT_F], F32, name="y%d" % grp)
             nc.sync.dma_start(out=y_t[:], in_=y_view[:, rows, :])
             g_t = loads.tile([P, T, OUT_F], BF16, name="g%d" % grp)
@@ -97,8 +98,8 @@ def tile_vdl_t_v_kernel(tc, x_in, w, b, y, grad_out, out):
         def columns(tiles, grp):
             return tiles[grp][:].rearrange("p i (j c) -> p i j c", c=PACK)
 
-        def new(name, grp, dtype=F32, shape=(P, T, WORDS)):
-            kept[name, grp] = work.tile(list(shape), dtype, name=name)
+        def new(name, grp, dtype=F32, inner=(WORDS,)):
+            kept[name, grp] = work.tile([P, SIZES[grp]] + list(inner), dtype, name=name)
             return kept[name, grp]
 
         def turns_of(grp):
@@ -128,7 +129,7 @@ def tile_vdl_t_v_kernel(tc, x_in, w, b, y, grad_out, out):
             )
 
         def relu_column(grp):
-            dy = new("dy", grp, BF16, (P, T, PACK, WORDS))
+            dy = new("dy", grp, BF16, (PACK, WORDS))
             nc.vector.scalar_tensor_tensor(
                 out=dy[:, :, 2, :], in0=columns(y_sb, grp)[:, :, :, 2], scalar=0.0,
                 in1=columns(g_sb, grp)[:, :, :, 2], op0=ALU.is_gt, op1=ALU.mult,
@@ -154,20 +155,20 @@ def tile_vdl_t_v_kernel(tc, x_in, w, b, y, grad_out, out):
 
         def transposes(grp):
             dy = kept["dy", grp]
-            dy_t = psum_t.tile([P, T, PACK, P], BF16, name="dy_t")
+            dy_t = psum_t.tile([P, SIZES[grp], PACK, P], BF16, name="dy_t")
             kept["dy_t", grp] = dy_t
-            for i in range(T):
+            for i in range(SIZES[grp]):
                 for c in range(PACK):
                     nc.tensor.transpose(dy_t[:, i, c, :], dy[:, i, c, :], ident[:])
 
         def interleave(grp):
-            grouped = work.tile([P, T, P, PACK], BF16, name="grouped", align_bytes=64)
+            grouped = work.tile([P, SIZES[grp], P, PACK], BF16, name="grouped", align_bytes=64)
             kept["grouped", grp] = grouped
             nc.scalar.copy(out=grouped[:], in_=kept["dy_t", grp][:].rearrange("p i c t -> p i t c"))
 
         def quantise(grp):
-            codes = mx.tile([P, T * P], U32, name="codes", align_bytes=64)
-            scales = mx.tile([P, T * P], U8, name="scales", align_bytes=64)
+            codes = mx.tile([P, SIZES[grp] * P], U32, name="codes", align_bytes=64)
+            scales = mx.tile([P, SIZES[grp] * P], U8, name="scales", align_bytes=64)
             nc.vector.quantize_mx(
                 out=codes[:].bitcast(E5M2X4),
                 scales=scales[:],
@@ -177,7 +178,7 @@ def tile_vdl_t_v_kernel(tc, x_in, w, b, y, grad_out, out):
 
         def multiply(grp):
             codes, scales = kept["codes", grp]
-            for i in range(T):
+            for i in range(SIZES[grp]):
                 toks = slice(i * P, (i + 1) * P)
                 for h, cols in enumerate(halves()):
                     acc = psum_o.tile([P, N_HALF], F32, name="acc")
@@ -193,15 +194,16 @@ def tile_vdl_t_v_kernel(tc, x_in, w, b, y, grad_out, out):
                     )
 
         def empty_and_store(grp):
-            for i in range(T):
+            for i in range(SIZES[grp]):
+                tile_no = FIRST[grp] + i
                 result = outs.tile([P, IN_F], F32, name="result")
                 for h, cols in enumerate(halves()):
                     acc = kept["acc", grp, i, h]
-                    if h == 0 and grp >= (VECTOR_ONE_FROM if i == 0 else VECTOR_TWO_FROM):
+                    if h == 0 and tile_no >= (VECTOR_EVEN_FROM if tile_no % 2 == 0 else VECTOR_ODD_FROM):
                         nc.vector.tensor_copy(out=result[:, cols], in_=acc[:])
                     else:
                         nc.scalar.copy(out=result[:, cols], in_=acc[:])
-                nc.sync.dma_start(out=out_view[:, grp * T + i, :], in_=result[:])
+                nc.sync.dma_start(out=out_view[:, tile_no, :], in_=result[:])
 
         def is_group(grp):
             return 0 <= grp < GROUPS

@@ -15,6 +15,7 @@ ALU = mybir.AluOpType
 
 P = 128
 PACK = 4
+PAIR = 2
 TOKENS = 2048
 OUT_F = 512
 IN_F = 1024
@@ -24,10 +25,9 @@ HALVES = IN_F // N_HALF
 TOK_PER_PART = TOKENS // P
 SIZES = (2, 2, 2, 2, 2, 2, 2, 1, 1)
 GROUPS = len(SIZES)
-
-VECTOR_EVEN_FROM = 2
-VECTOR_ODD_FROM = 5
-W_AFTER = 2
+SQUARES_ON_SCALAR = 3
+VECTOR_EVERY = 4
+VECTOR_FROM = 13
 
 ROUND_MAGIC = 12582912.0
 
@@ -41,6 +41,7 @@ def tile_vdl_t_v_kernel(tc, x_in, w, b, y, grad_out, out):
     y_view = y.rearrange("(q i) k -> q i k", i=TOK_PER_PART)
     g_view = grad_out.rearrange("(q i) k -> q i k", i=TOK_PER_PART)
     out_view = out.rearrange("(q i) n -> q i n", i=TOK_PER_PART)
+    w_view = w.rearrange("(p e u) n -> p u e n", e=PAIR, u=2)
 
     with ExitStack() as ctx:
         consts = ctx.enter_context(tc.tile_pool(name="consts", bufs=1))
@@ -51,6 +52,9 @@ def tile_vdl_t_v_kernel(tc, x_in, w, b, y, grad_out, out):
         psum_t = ctx.enter_context(tc.psum_pool(name="psum_t", bufs=2))
         psum_o = ctx.enter_context(tc.psum_pool(name="psum_o", bufs=6))
 
+        def half(h):
+            return slice(h * N_HALF, (h + 1) * N_HALF)
+
         y_sb = []
         g_sb = []
         w_raw = loads.tile([P, PACK, IN_F], BF16, name="w_raw")
@@ -58,53 +62,58 @@ def tile_vdl_t_v_kernel(tc, x_in, w, b, y, grad_out, out):
             rows = slice(FIRST[grp], FIRST[grp] + T)
             y_t = loads.tile([P, T, OUT_F], F32, name="y%d" % grp)
             nc.sync.dma_start(out=y_t[:], in_=y_view[:, rows, :])
+            if grp == 0:
+                for h in range(HALVES):
+                    for u in range(2):
+                        nc.sync.dma_start(
+                            out=w_raw[:, 2 * u : 2 * u + 2, half(h)], in_=w_view[:, u, :, half(h)]
+                        )
             g_t = loads.tile([P, T, OUT_F], BF16, name="g%d" % grp)
             nc.sync.dma_start(out=g_t[:], in_=g_view[:, rows, :])
             y_sb.append(y_t)
             g_sb.append(g_t)
-            if grp == W_AFTER:
-                nc.sync.dma_start(out=w_raw[:], in_=w.rearrange("(p j) n -> p j n", j=PACK))
 
         warm_in = consts.tile([P, 1], F32, name="warm_in")
         warm_out = consts.tile([P, 1], F32, name="warm_out")
         nc.vector.memset(warm_in[:], 0.0)
         nc.scalar.activation(out=warm_out[:], in_=warm_in[:], func=ACT.Silu)
 
-        ident = consts.tile([P, P], BF16, name="ident")
+        ident = consts.tile([P, P], F32, name="ident")
         make_identity(nc, ident[:])
 
         w_grouped = consts.tile([P, IN_F, PACK], BF16, name="w_grouped", align_bytes=64)
         w_codes = consts.tile([P, IN_F], U32, name="w_codes", align_bytes=64)
         w_scales = consts.tile([P, IN_F], U8, name="w_scales", align_bytes=64)
 
-        def halves():
-            return [slice(h * N_HALF, (h + 1) * N_HALF) for h in range(HALVES)]
+        def group_w(h):
+            nc.vector.tensor_scalar(
+                out=w_grouped[:, half(h), :].rearrange("p (c i) t -> p c t i", i=4),
+                in0=w_raw[:, :, half(h)].rearrange("p t (c i) -> p c t i", i=4),
+                scalar1=-1.0, scalar2=None, op0=ALU.mult,
+            )
 
-        def prepare_w():
-            for cols in halves():
-                nc.vector.tensor_copy(
-                    out=w_grouped[:, cols, :].rearrange("p (c i) t -> p c t i", i=4),
-                    in_=w_raw[:, :, cols].rearrange("p t (c i) -> p c t i", i=4),
-                )
-            for cols in halves():
-                nc.vector.quantize_mx(
-                    out=w_codes[:, cols].bitcast(E4M3X4),
-                    scales=w_scales[:, cols],
-                    in_=w_grouped[:, cols, :].rearrange("p n t -> p (n t)"),
-                )
+        def quantise_w(h):
+            nc.vector.quantize_mx(
+                out=w_codes[:, half(h)].bitcast(E4M3X4),
+                scales=w_scales[:, half(h)],
+                in_=w_grouped[:, half(h), :].rearrange("p n t -> p (n t)"),
+            )
 
         kept = {}
 
-        def columns(tiles, grp):
-            return tiles[grp][:].rearrange("p i (j c) -> p i j c", c=PACK)
+        def y_column(grp, c):
+            return y_sb[grp][:].rearrange("p i (j c) -> p i j c", c=PACK)[:, :, :, c]
 
-        def new(name, grp, dtype=F32, inner=(WORDS,)):
-            kept[name, grp] = work.tile([P, SIZES[grp]] + list(inner), dtype, name=name)
+        def g_pairs(grp, u):
+            return g_sb[grp][:].rearrange("p i (j e u) -> p (i j) e u", e=PAIR, u=2)[:, :, :, u]
+
+        def new(name, grp, lead=(), dtype=F32):
+            kept[name, grp] = work.tile([P] + list(lead) + [SIZES[grp], WORDS], dtype, name=name)
             return kept[name, grp]
 
         def turns_of(grp):
             nc.vector.tensor_scalar(
-                out=new("turns", grp)[:], in0=columns(y_sb, grp)[:, :, :, 1],
+                out=new("turns", grp)[:], in0=y_column(grp, 1),
                 scalar1=1.0 / (2.0 * math.pi), scalar2=0.25, op0=ALU.mult, op1=ALU.add,
             )
 
@@ -120,89 +129,101 @@ def tile_vdl_t_v_kernel(tc, x_in, w, b, y, grad_out, out):
                 op=ALU.subtract,
             )
 
-        def functions_of(grp):
-            y4 = columns(y_sb, grp)
-            nc.scalar.activation(out=new("th0", grp)[:], in_=y4[:, :, :, 0], func=ACT.Tanh)
-            nc.scalar.activation(out=new("th3", grp)[:], in_=y4[:, :, :, 3], func=ACT.Tanh, scale=0.5)
+        def tanh_of(grp):
+            new("parts", grp, (PACK,))
+            th = new("th", grp, (2,))
+            nc.scalar.activation(out=th[:, 0], in_=y_column(grp, 0), func=ACT.Tanh)
+            nc.scalar.activation(out=th[:, 1], in_=y_column(grp, 3), func=ACT.Tanh, scale=0.5)
+
+        def sin_of(grp):
             nc.scalar.activation(
-                out=new("cosy", grp)[:], in_=kept["frac", grp][:], func=ACT.Sin, scale=2.0 * math.pi
+                out=kept["parts", grp][:, 2], in_=kept["frac", grp][:], func=ACT.Sin, scale=-2.0 * math.pi
             )
 
-        def relu_column(grp):
-            dy = new("dy", grp, BF16, (PACK, WORDS))
+        def squares(grp):
+            th = kept["th", grp]
+            sq = kept["parts", grp][:, 0:PACK:3]
+            if grp < SQUARES_ON_SCALAR:
+                nc.scalar.activation(out=sq, in_=th[:], func=ACT.Square)
+            else:
+                nc.vector.tensor_tensor(out=sq, in0=th[:], in1=th[:], op=ALU.mult)
+
+        def not_positive(grp):
+            nc.vector.tensor_scalar(
+                out=kept["parts", grp][:, 1], in0=y_column(grp, 2), scalar1=0.0, scalar2=None, op0=ALU.is_le
+            )
+
+        def minus_sigmoid(grp):
+            part = kept["parts", grp][:, 3]
+            nc.vector.tensor_scalar(
+                out=part, in0=part, scalar1=0.25, scalar2=-0.25, op0=ALU.mult, op1=ALU.add
+            )
+
+        def tanh_and_relu(grp):
+            dy = work.tile([P, 2, SIZES[grp] * WORDS, PAIR], BF16, name="dy")
+            kept["dy", grp] = dy
             nc.vector.scalar_tensor_tensor(
-                out=dy[:, :, 2, :], in0=columns(y_sb, grp)[:, :, :, 2], scalar=0.0,
-                in1=columns(g_sb, grp)[:, :, :, 2], op0=ALU.is_gt, op1=ALU.mult,
+                out=dy[:, 0], in0=kept["parts", grp][:, 0:2].rearrange("p e i j -> p (i j) e"), scalar=1.0,
+                in1=g_pairs(grp, 0), op0=ALU.subtract, op1=ALU.mult,
             )
 
-        def minus_square(grp, name, source, factor):
-            th = kept[source, grp]
-            nc.vector.scalar_tensor_tensor(
-                out=new(name, grp)[:], in0=th[:], scalar=-factor, in1=th[:], op0=ALU.mult, op1=ALU.mult
-            )
-
-        def squared_column(grp, c, name, factor):
-            nc.vector.scalar_tensor_tensor(
-                out=kept["dy", grp][:, :, c, :], in0=kept[name, grp][:], scalar=factor,
-                in1=columns(g_sb, grp)[:, :, :, c], op0=ALU.add, op1=ALU.mult,
-            )
-
-        def cos_column(grp):
+        def sin_and_sigmoid(grp):
             nc.vector.tensor_tensor(
-                out=kept["dy", grp][:, :, 1, :], in0=kept["cosy", grp][:],
-                in1=columns(g_sb, grp)[:, :, :, 1], op=ALU.mult,
+                out=kept["dy", grp][:, 1], in0=kept["parts", grp][:, 2:4].rearrange("p e i j -> p (i j) e"),
+                in1=g_pairs(grp, 1), op=ALU.mult,
             )
 
         def transposes(grp):
             dy = kept["dy", grp]
-            dy_t = psum_t.tile([P, SIZES[grp], PACK, P], BF16, name="dy_t")
+            dy_t = psum_t.tile([P, SIZES[grp], 2, P], F32, name="dy_t")
             kept["dy_t", grp] = dy_t
             for i in range(SIZES[grp]):
-                for c in range(PACK):
-                    nc.tensor.transpose(dy_t[:, i, c, :], dy[:, i, c, :], ident[:])
+                for u in range(2):
+                    words = dy[:, u, i * WORDS : (i + 1) * WORDS, :].rearrange("p j e -> p (j e)").bitcast(F32)
+                    nc.tensor.transpose(dy_t[:, i, u, :], words, ident[:])
 
         def interleave(grp):
-            grouped = work.tile([P, SIZES[grp], P, PACK], BF16, name="grouped", align_bytes=64)
+            grouped = work.tile([P, SIZES[grp] * P * PACK], BF16, name="grouped", align_bytes=64)
             kept["grouped", grp] = grouped
-            nc.scalar.copy(out=grouped[:], in_=kept["dy_t", grp][:].rearrange("p i c t -> p i t c"))
+            nc.scalar.copy(
+                out=grouped[:].bitcast(F32).rearrange("p (i t u) -> p i t u", i=SIZES[grp], u=2),
+                in_=kept["dy_t", grp][:].rearrange("p i u t -> p i t u"),
+            )
 
         def quantise(grp):
             codes = mx.tile([P, SIZES[grp] * P], U32, name="codes", align_bytes=64)
             scales = mx.tile([P, SIZES[grp] * P], U8, name="scales", align_bytes=64)
-            nc.vector.quantize_mx(
-                out=codes[:].bitcast(E5M2X4),
-                scales=scales[:],
-                in_=kept["grouped", grp][:].rearrange("p i t c -> p (i t c)"),
-            )
+            nc.vector.quantize_mx(out=codes[:].bitcast(E5M2X4), scales=scales[:], in_=kept["grouped", grp][:])
             kept["codes", grp] = (codes, scales)
 
         def multiply(grp):
             codes, scales = kept["codes", grp]
             for i in range(SIZES[grp]):
                 toks = slice(i * P, (i + 1) * P)
-                for h, cols in enumerate(halves()):
+                for h in range(HALVES):
                     acc = psum_o.tile([P, N_HALF], F32, name="acc")
                     kept["acc", grp, i, h] = acc
                     nc.tensor.matmul_mx(
                         out=acc[:],
                         lhsT=codes[:, toks].bitcast(E5M2X4),
                         lhsT_scale=scales[:, toks],
-                        rhs=w_codes[:, cols].bitcast(E4M3X4),
-                        rhs_scale=w_scales[:, cols],
+                        rhs=w_codes[:, half(h)].bitcast(E4M3X4),
+                        rhs_scale=w_scales[:, half(h)],
                         start=True,
                         stop=True,
                     )
 
-        def empty_and_store(grp):
-            for i in range(SIZES[grp]):
-                tile_no = FIRST[grp] + i
-                result = outs.tile([P, IN_F], F32, name="result")
-                for h, cols in enumerate(halves()):
-                    acc = kept["acc", grp, i, h]
-                    if h == 0 and tile_no >= (VECTOR_EVEN_FROM if tile_no % 2 == 0 else VECTOR_ODD_FROM):
-                        nc.vector.tensor_copy(out=result[:, cols], in_=acc[:])
-                    else:
-                        nc.scalar.copy(out=result[:, cols], in_=acc[:])
+        def empty(grp, i, h):
+            tile_no = FIRST[grp] + i
+            if h == 0:
+                kept["result", grp, i] = outs.tile([P, IN_F], F32, name="result")
+            result = kept["result", grp, i]
+            acc = kept["acc", grp, i, h]
+            if h == 0 and (tile_no >= VECTOR_FROM or tile_no % VECTOR_EVERY == 2):
+                nc.vector.tensor_copy(out=result[:, half(h)], in_=acc[:])
+            else:
+                nc.scalar.copy(out=result[:, half(h)], in_=acc[:])
+            if h == HALVES - 1:
                 nc.sync.dma_start(out=out_view[:, tile_no, :], in_=result[:])
 
         def is_group(grp):
@@ -212,33 +233,50 @@ def tile_vdl_t_v_kernel(tc, x_in, w, b, y, grad_out, out):
             turns_of(0)
             whole_of(0)
             frac_of(0)
-            functions_of(0)
+            tanh_of(0)
+            sin_of(0)
+            squares(0)
+            group_w(0)
+            group_w(1)
             for r in range(GROUPS + 2):
-                if r == W_AFTER:
-                    prepare_w()
-                if is_group(r - 2):
-                    quantise(r - 2)
-                    multiply(r - 2)
-                if is_group(r - 1):
-                    interleave(r - 1)
                 ahead = is_group(r + 1)
+                behind = is_group(r - 2)
                 if is_group(r):
-                    relu_column(r)
+                    if r >= SQUARES_ON_SCALAR:
+                        squares(r)
+                    not_positive(r)
                 if ahead:
                     turns_of(r + 1)
+                    tanh_of(r + 1)
+                if is_group(r - 1):
+                    interleave(r - 1)
                 if is_group(r):
-                    minus_square(r, "nsq0", "th0", 1.0)
+                    minus_sigmoid(r)
                 if ahead:
                     whole_of(r + 1)
+                if behind:
+                    empty(r - 2, 0, 0)
                 if is_group(r):
-                    minus_square(r, "nsq3", "th3", 0.25)
+                    tanh_and_relu(r)
+                if r == 0:
+                    quantise_w(0)
                 if ahead:
                     frac_of(r + 1)
-                    functions_of(r + 1)
+                if behind:
+                    empty(r - 2, 0, 1)
+                if ahead:
+                    sin_of(r + 1)
+                    if r + 1 < SQUARES_ON_SCALAR:
+                        squares(r + 1)
+                if behind and SIZES[r - 2] > 1:
+                    empty(r - 2, 1, 0)
+                if r == 0:
+                    quantise_w(1)
                 if is_group(r):
-                    squared_column(r, 0, "nsq0", 1.0)
-                    squared_column(r, 3, "nsq3", 0.25)
-                    cos_column(r)
+                    sin_and_sigmoid(r)
                     transposes(r)
-                if is_group(r - 2):
-                    empty_and_store(r - 2)
+                if is_group(r - 1):
+                    quantise(r - 1)
+                    multiply(r - 1)
+                if behind and SIZES[r - 2] > 1:
+                    empty(r - 2, 1, 1)

@@ -23,11 +23,12 @@ WORDS = OUT_F // PACK
 N_HALF = 512
 HALVES = IN_F // N_HALF
 TOK_PER_PART = TOKENS // P
-SIZES = (2, 2, 2, 2, 2, 2, 2, 1, 1)
+SIZES = (1, 1, 2, 2, 2, 2, 2, 2, 1, 1)
 GROUPS = len(SIZES)
-SQUARES_ON_SCALAR = 3
-VECTOR_EVERY = 4
-VECTOR_FROM = 13
+W_BEHIND_Y = 1
+SQUARES_ON_SCALAR = 5
+VECTOR_EVEN_FROM = 8
+VECTOR_ODD_FROM = 12
 
 ROUND_MAGIC = 12582912.0
 
@@ -57,17 +58,17 @@ def tile_vdl_t_v_kernel(tc, x_in, w, b, y, grad_out, out):
 
         y_sb = []
         g_sb = []
-        w_raw = loads.tile([P, PACK, IN_F], BF16, name="w_raw")
+        w_raw = []
         for grp, T in enumerate(SIZES):
             rows = slice(FIRST[grp], FIRST[grp] + T)
             y_t = loads.tile([P, T, OUT_F], F32, name="y%d" % grp)
             nc.sync.dma_start(out=y_t[:], in_=y_view[:, rows, :])
-            if grp == 0:
+            if grp == W_BEHIND_Y:
                 for h in range(HALVES):
+                    w_half = loads.tile([P, PACK, N_HALF], BF16, name="w%d" % h)
                     for u in range(2):
-                        nc.sync.dma_start(
-                            out=w_raw[:, 2 * u : 2 * u + 2, half(h)], in_=w_view[:, u, :, half(h)]
-                        )
+                        nc.sync.dma_start(out=w_half[:, 2 * u : 2 * u + 2, :], in_=w_view[:, u, :, half(h)])
+                    w_raw.append(w_half)
             g_t = loads.tile([P, T, OUT_F], BF16, name="g%d" % grp)
             nc.sync.dma_start(out=g_t[:], in_=g_view[:, rows, :])
             y_sb.append(y_t)
@@ -86,11 +87,12 @@ def tile_vdl_t_v_kernel(tc, x_in, w, b, y, grad_out, out):
         w_scales = consts.tile([P, IN_F], U8, name="w_scales", align_bytes=64)
 
         def group_w(h):
-            nc.vector.tensor_scalar(
-                out=w_grouped[:, half(h), :].rearrange("p (c i) t -> p c t i", i=4),
-                in0=w_raw[:, :, half(h)].rearrange("p t (c i) -> p c t i", i=4),
-                scalar1=-1.0, scalar2=None, op0=ALU.mult,
-            )
+            grouped = w_grouped[:, half(h), :].rearrange("p (c i) t -> p c t i", i=4)
+            raw = w_raw[h][:].rearrange("p t (c i) -> p c t i", i=4)
+            if h == 0:
+                nc.vector.tensor_scalar(out=grouped, in0=raw, scalar1=-1.0, scalar2=None, op0=ALU.mult)
+            else:
+                nc.scalar.activation(out=grouped, in_=raw, func=ACT.Copy, scale=-1.0)
 
         def quantise_w(h):
             nc.vector.quantize_mx(
@@ -129,47 +131,56 @@ def tile_vdl_t_v_kernel(tc, x_in, w, b, y, grad_out, out):
                 op=ALU.subtract,
             )
 
+        def compact(grp):
+            pair = work.tile([P, SIZES[grp] * WORDS, PAIR], F32, name="pair")
+            kept["pair", grp] = pair
+            nc.vector.tensor_copy(
+                out=pair[:], in_=y_sb[grp][:].rearrange("p i (j c) -> p (i j) c", c=PACK)[:, :, 0:PACK:3]
+            )
+
         def tanh_of(grp):
-            new("parts", grp, (PACK,))
+            new("wave", grp, (2,))
             th = new("th", grp, (2,))
-            nc.scalar.activation(out=th[:, 0], in_=y_column(grp, 0), func=ACT.Tanh)
-            nc.scalar.activation(out=th[:, 1], in_=y_column(grp, 3), func=ACT.Tanh, scale=0.5)
+            pair = kept["pair", grp][:].rearrange("p (i j) e -> p i j e", i=SIZES[grp])
+            nc.scalar.activation(out=th[:, 0], in_=pair[:, :, :, 1], func=ACT.Tanh, scale=0.5)
+            nc.scalar.activation(out=th[:, 1], in_=pair[:, :, :, 0], func=ACT.Tanh)
 
         def sin_of(grp):
             nc.scalar.activation(
-                out=kept["parts", grp][:, 2], in_=kept["frac", grp][:], func=ACT.Sin, scale=-2.0 * math.pi
+                out=kept["wave", grp][:, 0], in_=kept["frac", grp][:], func=ACT.Sin, scale=-2.0 * math.pi
             )
 
         def squares(grp):
             th = kept["th", grp]
-            sq = kept["parts", grp][:, 0:PACK:3]
+            sq = kept["flat", grp][:, 0:2]
             if grp < SQUARES_ON_SCALAR:
                 nc.scalar.activation(out=sq, in_=th[:], func=ACT.Square)
             else:
                 nc.vector.tensor_tensor(out=sq, in0=th[:], in1=th[:], op=ALU.mult)
 
         def not_positive(grp):
+            new("flat", grp, (3,))
             nc.vector.tensor_scalar(
-                out=kept["parts", grp][:, 1], in0=y_column(grp, 2), scalar1=0.0, scalar2=None, op0=ALU.is_le
+                out=kept["flat", grp][:, 2], in0=y_column(grp, 2), scalar1=0.0, scalar2=None, op0=ALU.is_le
             )
 
         def minus_sigmoid(grp):
-            part = kept["parts", grp][:, 3]
             nc.vector.tensor_scalar(
-                out=part, in0=part, scalar1=0.25, scalar2=-0.25, op0=ALU.mult, op1=ALU.add
+                out=kept["wave", grp][:, 1], in0=kept["flat", grp][:, 0], scalar1=0.25, scalar2=-0.25,
+                op0=ALU.mult, op1=ALU.add,
             )
 
         def tanh_and_relu(grp):
             dy = work.tile([P, 2, SIZES[grp] * WORDS, PAIR], BF16, name="dy")
             kept["dy", grp] = dy
             nc.vector.scalar_tensor_tensor(
-                out=dy[:, 0], in0=kept["parts", grp][:, 0:2].rearrange("p e i j -> p (i j) e"), scalar=1.0,
+                out=dy[:, 0], in0=kept["flat", grp][:, 1:3].rearrange("p e i j -> p (i j) e"), scalar=1.0,
                 in1=g_pairs(grp, 0), op0=ALU.subtract, op1=ALU.mult,
             )
 
         def sin_and_sigmoid(grp):
             nc.vector.tensor_tensor(
-                out=kept["dy", grp][:, 1], in0=kept["parts", grp][:, 2:4].rearrange("p e i j -> p (i j) e"),
+                out=kept["dy", grp][:, 1], in0=kept["wave", grp][:].rearrange("p e i j -> p (i j) e"),
                 in1=g_pairs(grp, 1), op=ALU.mult,
             )
 
@@ -215,15 +226,16 @@ def tile_vdl_t_v_kernel(tc, x_in, w, b, y, grad_out, out):
 
         def empty(grp, i, h):
             tile_no = FIRST[grp] + i
-            if h == 0:
+            store = ("result", grp, i) in kept
+            if not store:
                 kept["result", grp, i] = outs.tile([P, IN_F], F32, name="result")
             result = kept["result", grp, i]
             acc = kept["acc", grp, i, h]
-            if h == 0 and (tile_no >= VECTOR_FROM or tile_no % VECTOR_EVERY == 2):
+            if h == 0 and tile_no >= (VECTOR_EVEN_FROM if tile_no % 2 == 0 else VECTOR_ODD_FROM):
                 nc.vector.tensor_copy(out=result[:, half(h)], in_=acc[:])
             else:
                 nc.scalar.copy(out=result[:, half(h)], in_=acc[:])
-            if h == HALVES - 1:
+            if store:
                 nc.sync.dma_start(out=out_view[:, tile_no, :], in_=result[:])
 
         def is_group(grp):
@@ -231,21 +243,21 @@ def tile_vdl_t_v_kernel(tc, x_in, w, b, y, grad_out, out):
 
         with tc.manual_schedule():
             turns_of(0)
+            compact(0)
             whole_of(0)
+            not_positive(0)
             frac_of(0)
             tanh_of(0)
             sin_of(0)
             squares(0)
-            group_w(0)
-            group_w(1)
             for r in range(GROUPS + 2):
                 ahead = is_group(r + 1)
                 behind = is_group(r - 2)
                 if is_group(r):
                     if r >= SQUARES_ON_SCALAR:
                         squares(r)
-                    not_positive(r)
                 if ahead:
+                    compact(r + 1)
                     turns_of(r + 1)
                     tanh_of(r + 1)
                 if is_group(r - 1):
@@ -254,29 +266,31 @@ def tile_vdl_t_v_kernel(tc, x_in, w, b, y, grad_out, out):
                     minus_sigmoid(r)
                 if ahead:
                     whole_of(r + 1)
-                if behind:
-                    empty(r - 2, 0, 0)
                 if is_group(r):
                     tanh_and_relu(r)
-                if r == 0:
-                    quantise_w(0)
                 if ahead:
                     frac_of(r + 1)
                 if behind:
                     empty(r - 2, 0, 1)
                 if ahead:
                     sin_of(r + 1)
+                    not_positive(r + 1)
                     if r + 1 < SQUARES_ON_SCALAR:
                         squares(r + 1)
-                if behind and SIZES[r - 2] > 1:
-                    empty(r - 2, 1, 0)
-                if r == 0:
-                    quantise_w(1)
                 if is_group(r):
                     sin_and_sigmoid(r)
                     transposes(r)
+                if r == 0:
+                    group_w(0)
+                    group_w(1)
+                    quantise_w(0)
                 if is_group(r - 1):
+                    if r == 1:
+                        quantise_w(1)
                     quantise(r - 1)
                     multiply(r - 1)
-                if behind and SIZES[r - 2] > 1:
-                    empty(r - 2, 1, 1)
+                if behind:
+                    empty(r - 2, 0, 0)
+                    if SIZES[r - 2] > 1:
+                        empty(r - 2, 1, 0)
+                        empty(r - 2, 1, 1)

@@ -23,10 +23,11 @@ WORDS = OUT_F // PACK
 N_HALF = 512
 HALVES = IN_F // N_HALF
 TOK_PER_PART = TOKENS // P
-SIZES = (1, 1, 2, 2, 2, 2, 2, 2, 1, 1)
+SIZES = (1, 2, 2, 2, 2, 2, 2, 2, 1)
 GROUPS = len(SIZES)
+BANK_TOKENS = 2
 W_BEHIND_Y = 1
-SQUARES_ON_SCALAR = 5
+SQUARES_ON_SCALAR = 4
 VECTOR_EVEN_FROM = 8
 VECTOR_ODD_FROM = 12
 
@@ -150,10 +151,13 @@ def tile_vdl_t_v_kernel(tc, x_in, w, b, y, grad_out, out):
                 out=kept["wave", grp][:, 0], in_=kept["frac", grp][:], func=ACT.Sin, scale=-2.0 * math.pi
             )
 
+        def on_scalar(grp):
+            return grp < SQUARES_ON_SCALAR
+
         def squares(grp):
             th = kept["th", grp]
             sq = kept["flat", grp][:, 0:2]
-            if grp < SQUARES_ON_SCALAR:
+            if on_scalar(grp):
                 nc.scalar.activation(out=sq, in_=th[:], func=ACT.Square)
             else:
                 nc.vector.tensor_tensor(out=sq, in0=th[:], in1=th[:], op=ALU.mult)
@@ -186,20 +190,25 @@ def tile_vdl_t_v_kernel(tc, x_in, w, b, y, grad_out, out):
 
         def transposes(grp):
             dy = kept["dy", grp]
-            dy_t = psum_t.tile([P, SIZES[grp], 2, P], F32, name="dy_t")
-            kept["dy_t", grp] = dy_t
             for i in range(SIZES[grp]):
+                if i % BANK_TOKENS == 0:
+                    dy_t = psum_t.tile([P, min(BANK_TOKENS, SIZES[grp]), 2, P], F32, name="dy_t")
+                    kept["dy_t", grp, i // BANK_TOKENS] = dy_t
                 for u in range(2):
                     words = dy[:, u, i * WORDS : (i + 1) * WORDS, :].rearrange("p j e -> p (j e)").bitcast(F32)
-                    nc.tensor.transpose(dy_t[:, i, u, :], words, ident[:])
+                    nc.tensor.transpose(dy_t[:, i % BANK_TOKENS, u, :], words, ident[:])
 
         def interleave(grp):
             grouped = work.tile([P, SIZES[grp] * P * PACK], BF16, name="grouped", align_bytes=64)
             kept["grouped", grp] = grouped
-            nc.scalar.copy(
-                out=grouped[:].bitcast(F32).rearrange("p (i t u) -> p i t u", i=SIZES[grp], u=2),
-                in_=kept["dy_t", grp][:].rearrange("p i u t -> p i t u"),
-            )
+            for i in range(0, SIZES[grp], BANK_TOKENS):
+                T = min(BANK_TOKENS, SIZES[grp])
+                nc.scalar.copy(
+                    out=grouped[:, i * P * PACK : (i + T) * P * PACK].bitcast(F32).rearrange(
+                        "p (i t u) -> p i t u", i=T, u=2
+                    ),
+                    in_=kept["dy_t", grp, i // BANK_TOKENS][:].rearrange("p i u t -> p i t u"),
+                )
 
         def quantise(grp):
             codes = mx.tile([P, SIZES[grp] * P], U32, name="codes", align_bytes=64)
@@ -224,6 +233,10 @@ def tile_vdl_t_v_kernel(tc, x_in, w, b, y, grad_out, out):
                         stop=True,
                     )
 
+        def on_vector(grp, i):
+            tile_no = FIRST[grp] + i
+            return tile_no >= (VECTOR_EVEN_FROM if tile_no % 2 == 0 else VECTOR_ODD_FROM)
+
         def empty(grp, i, h):
             tile_no = FIRST[grp] + i
             store = ("result", grp, i) in kept
@@ -231,7 +244,7 @@ def tile_vdl_t_v_kernel(tc, x_in, w, b, y, grad_out, out):
                 kept["result", grp, i] = outs.tile([P, IN_F], F32, name="result")
             result = kept["result", grp, i]
             acc = kept["acc", grp, i, h]
-            if h == 0 and tile_no >= (VECTOR_EVEN_FROM if tile_no % 2 == 0 else VECTOR_ODD_FROM):
+            if h == 0 and on_vector(grp, i):
                 nc.vector.tensor_copy(out=result[:, half(h)], in_=acc[:])
             else:
                 nc.scalar.copy(out=result[:, half(h)], in_=acc[:])
@@ -249,48 +262,57 @@ def tile_vdl_t_v_kernel(tc, x_in, w, b, y, grad_out, out):
             frac_of(0)
             tanh_of(0)
             sin_of(0)
-            squares(0)
+            if on_scalar(0):
+                squares(0)
             for r in range(GROUPS + 2):
                 ahead = is_group(r + 1)
                 behind = is_group(r - 2)
-                if is_group(r):
-                    if r >= SQUARES_ON_SCALAR:
-                        squares(r)
-                if ahead:
-                    compact(r + 1)
-                    turns_of(r + 1)
-                    tanh_of(r + 1)
                 if is_group(r - 1):
                     interleave(r - 1)
-                if is_group(r):
-                    minus_sigmoid(r)
+                if is_group(r) and not on_scalar(r):
+                    squares(r)
+                if ahead:
+                    compact(r + 1)
+                if ahead:
+                    tanh_of(r + 1)
+                if behind:
+                    empty(r - 2, 0, 1)
+                if ahead:
+                    turns_of(r + 1)
+                if ahead:
+                    not_positive(r + 1)
                 if ahead:
                     whole_of(r + 1)
+                if is_group(r):
+                    minus_sigmoid(r)
                 if is_group(r):
                     tanh_and_relu(r)
                 if ahead:
                     frac_of(r + 1)
-                if behind:
-                    empty(r - 2, 0, 1)
                 if ahead:
                     sin_of(r + 1)
-                    not_positive(r + 1)
-                    if r + 1 < SQUARES_ON_SCALAR:
-                        squares(r + 1)
+                if ahead and on_scalar(r + 1):
+                    squares(r + 1)
+                if r == 0:
+                    group_w(1)
+                if behind and not on_vector(r - 2, 0):
+                    empty(r - 2, 0, 0)
+                if behind and SIZES[r - 2] > 1 and not on_vector(r - 2, 1):
+                    empty(r - 2, 1, 0)
+                if behind and SIZES[r - 2] > 1:
+                    empty(r - 2, 1, 1)
                 if is_group(r):
                     sin_and_sigmoid(r)
                     transposes(r)
                 if r == 0:
                     group_w(0)
-                    group_w(1)
                     quantise_w(0)
+                if r == 1:
+                    quantise_w(1)
                 if is_group(r - 1):
-                    if r == 1:
-                        quantise_w(1)
                     quantise(r - 1)
                     multiply(r - 1)
-                if behind:
+                if behind and on_vector(r - 2, 0):
                     empty(r - 2, 0, 0)
-                    if SIZES[r - 2] > 1:
-                        empty(r - 2, 1, 0)
-                        empty(r - 2, 1, 1)
+                if behind and SIZES[r - 2] > 1 and on_vector(r - 2, 1):
+                    empty(r - 2, 1, 0)

@@ -25,13 +25,16 @@ HALVES = IN_F // N_HALF
 TOK_PER_PART = TOKENS // P
 SIZES = (1, 2, 2, 2, 2, 2, 2, 2, 1)
 GROUPS = len(SIZES)
+CHUNKS = (1, 1, 1, 2, 2, 2)
 BANK_TOKENS = 2
 W_BEHIND_Y = 1
 SQUARES_ON_SCALAR = 4
 VECTOR_EVEN_FROM = 8
-VECTOR_ODD_FROM = 12
+VECTOR_ODD_FROM = 99
 
 ROUND_MAGIC = 12582912.0
+
+PAIRED_STORES = 5
 
 FLOPS = 2 * TOKENS * OUT_F * IN_F
 BYTES = TOKENS * OUT_F * 4 + TOKENS * OUT_F * 2 + OUT_F * IN_F * 2 + TOKENS * IN_F * 4
@@ -60,20 +63,25 @@ def tile_vdl_t_v_kernel(tc, x_in, w, b, y, grad_out, out):
         y_sb = []
         g_sb = []
         w_raw = []
-        for grp, T in enumerate(SIZES):
-            rows = slice(FIRST[grp], FIRST[grp] + T)
-            y_t = loads.tile([P, T, OUT_F], F32, name="y%d" % grp)
+        done = 0
+        for k, chunk in enumerate(CHUNKS):
+            T = sum(SIZES[done : done + chunk])
+            rows = slice(FIRST[done], FIRST[done] + T)
+            y_t = loads.tile([P, T, OUT_F], F32, name="y%d" % k)
             nc.sync.dma_start(out=y_t[:], in_=y_view[:, rows, :])
-            if grp == W_BEHIND_Y:
+            if k == W_BEHIND_Y:
                 for h in range(HALVES):
                     w_half = loads.tile([P, PACK, N_HALF], BF16, name="w%d" % h)
                     for u in range(2):
                         nc.sync.dma_start(out=w_half[:, 2 * u : 2 * u + 2, :], in_=w_view[:, u, :, half(h)])
                     w_raw.append(w_half)
-            g_t = loads.tile([P, T, OUT_F], BF16, name="g%d" % grp)
+            g_t = loads.tile([P, T, OUT_F], BF16, name="g%d" % k)
             nc.sync.dma_start(out=g_t[:], in_=g_view[:, rows, :])
-            y_sb.append(y_t)
-            g_sb.append(g_t)
+            for grp in range(done, done + chunk):
+                own = slice(FIRST[grp] - FIRST[done], FIRST[grp] - FIRST[done] + SIZES[grp])
+                y_sb.append(y_t[:, own, :])
+                g_sb.append(g_t[:, own, :])
+            done += chunk
 
         warm_in = consts.tile([P, 1], F32, name="warm_in")
         warm_out = consts.tile([P, 1], F32, name="warm_out")
@@ -105,10 +113,10 @@ def tile_vdl_t_v_kernel(tc, x_in, w, b, y, grad_out, out):
         kept = {}
 
         def y_column(grp, c):
-            return y_sb[grp][:].rearrange("p i (j c) -> p i j c", c=PACK)[:, :, :, c]
+            return y_sb[grp].rearrange("p i (j c) -> p i j c", c=PACK)[:, :, :, c]
 
         def g_pairs(grp, u):
-            return g_sb[grp][:].rearrange("p i (j e u) -> p (i j) e u", e=PAIR, u=2)[:, :, :, u]
+            return g_sb[grp].rearrange("p i (j e u) -> p (i j) e u", e=PAIR, u=2)[:, :, :, u]
 
         def new(name, grp, lead=(), dtype=F32):
             kept[name, grp] = work.tile([P] + list(lead) + [SIZES[grp], WORDS], dtype, name=name)
@@ -136,7 +144,7 @@ def tile_vdl_t_v_kernel(tc, x_in, w, b, y, grad_out, out):
             pair = work.tile([P, SIZES[grp] * WORDS, PAIR], F32, name="pair")
             kept["pair", grp] = pair
             nc.vector.tensor_copy(
-                out=pair[:], in_=y_sb[grp][:].rearrange("p i (j c) -> p (i j) c", c=PACK)[:, :, 0:PACK:3]
+                out=pair[:], in_=y_sb[grp].rearrange("p i (j c) -> p (i j) c", c=PACK)[:, :, 0:PACK:3]
             )
 
         def tanh_of(grp):
@@ -238,18 +246,22 @@ def tile_vdl_t_v_kernel(tc, x_in, w, b, y, grad_out, out):
             return tile_no >= (VECTOR_EVEN_FROM if tile_no % 2 == 0 else VECTOR_ODD_FROM)
 
         def empty(grp, i, h):
-            tile_no = FIRST[grp] + i
-            store = ("result", grp, i) in kept
-            if not store:
-                kept["result", grp, i] = outs.tile([P, IN_F], F32, name="result")
-            result = kept["result", grp, i]
+            together = SIZES[grp] if grp < PAIRED_STORES else 1
+            key = ("result", grp, i // together)
+            if key not in kept:
+                kept[key] = outs.tile([P, together, IN_F], F32, name="result")
+                kept["left", key] = [together * HALVES]
+            result = kept[key]
             acc = kept["acc", grp, i, h]
+            place = result[:, i % together, half(h)]
             if h == 0 and on_vector(grp, i):
-                nc.vector.tensor_copy(out=result[:, half(h)], in_=acc[:])
+                nc.vector.tensor_copy(out=place, in_=acc[:])
             else:
-                nc.scalar.copy(out=result[:, half(h)], in_=acc[:])
-            if store:
-                nc.sync.dma_start(out=out_view[:, tile_no, :], in_=result[:])
+                nc.scalar.copy(out=place, in_=acc[:])
+            kept["left", key][0] -= 1
+            if kept["left", key][0] == 0:
+                first = FIRST[grp] + i // together * together
+                nc.sync.dma_start(out=out_view[:, first : first + together, :], in_=result[:])
 
         def is_group(grp):
             return 0 <= grp < GROUPS
@@ -275,35 +287,23 @@ def tile_vdl_t_v_kernel(tc, x_in, w, b, y, grad_out, out):
                     compact(r + 1)
                 if ahead:
                     tanh_of(r + 1)
+                if behind and not on_vector(r - 2, 0):
+                    empty(r - 2, 0, 0)
                 if behind:
                     empty(r - 2, 0, 1)
                 if ahead:
                     turns_of(r + 1)
-                if ahead:
-                    not_positive(r + 1)
-                if ahead:
-                    whole_of(r + 1)
                 if is_group(r):
                     minus_sigmoid(r)
                 if is_group(r):
                     tanh_and_relu(r)
                 if ahead:
-                    frac_of(r + 1)
-                if ahead:
-                    sin_of(r + 1)
-                if ahead and on_scalar(r + 1):
-                    squares(r + 1)
-                if r == 0:
-                    group_w(1)
-                if behind and not on_vector(r - 2, 0):
-                    empty(r - 2, 0, 0)
-                if behind and SIZES[r - 2] > 1 and not on_vector(r - 2, 1):
-                    empty(r - 2, 1, 0)
-                if behind and SIZES[r - 2] > 1:
-                    empty(r - 2, 1, 1)
+                    whole_of(r + 1)
                 if is_group(r):
                     sin_and_sigmoid(r)
                     transposes(r)
+                if ahead:
+                    frac_of(r + 1)
                 if r == 0:
                     group_w(0)
                     quantise_w(0)
@@ -312,6 +312,18 @@ def tile_vdl_t_v_kernel(tc, x_in, w, b, y, grad_out, out):
                 if is_group(r - 1):
                     quantise(r - 1)
                     multiply(r - 1)
+                if ahead:
+                    not_positive(r + 1)
+                if ahead and on_scalar(r + 1):
+                    squares(r + 1)
+                if r == 0:
+                    group_w(1)
+                if behind and SIZES[r - 2] > 1 and not on_vector(r - 2, 1):
+                    empty(r - 2, 1, 0)
+                if ahead:
+                    sin_of(r + 1)
+                if behind and SIZES[r - 2] > 1:
+                    empty(r - 2, 1, 1)
                 if behind and on_vector(r - 2, 0):
                     empty(r - 2, 0, 0)
                 if behind and SIZES[r - 2] > 1 and on_vector(r - 2, 1):

@@ -23,18 +23,15 @@ WORDS = OUT_F // PACK
 N_HALF = 512
 HALVES = IN_F // N_HALF
 TOK_PER_PART = TOKENS // P
-SIZES = (1, 2, 2, 2, 2, 2, 2, 2, 1)
+SIZES = (1, 2, 2, 2, 2, 2, 2, 1, 1, 1)
 GROUPS = len(SIZES)
-CHUNKS = (1, 1, 1, 2, 2, 2)
-BANK_TOKENS = 2
+CHUNKS = (1, 1, 1, 2, 2, 3)
 W_BEHIND_Y = 1
 SQUARES_ON_SCALAR = 4
-VECTOR_EVEN_FROM = 8
-VECTOR_ODD_FROM = 99
+VECTOR_EVEN_FROM = 6
+VECTOR_ODD_FROM = 15
 
 ROUND_MAGIC = 12582912.0
-
-PAIRED_STORES = 5
 
 FLOPS = 2 * TOKENS * OUT_F * IN_F
 BYTES = TOKENS * OUT_F * 4 + TOKENS * OUT_F * 2 + OUT_F * IN_F * 2 + TOKENS * IN_F * 4
@@ -198,25 +195,20 @@ def tile_vdl_t_v_kernel(tc, x_in, w, b, y, grad_out, out):
 
         def transposes(grp):
             dy = kept["dy", grp]
+            dy_t = psum_t.tile([P, SIZES[grp], 2, P], F32, name="dy_t")
+            kept["dy_t", grp] = dy_t
             for i in range(SIZES[grp]):
-                if i % BANK_TOKENS == 0:
-                    dy_t = psum_t.tile([P, min(BANK_TOKENS, SIZES[grp]), 2, P], F32, name="dy_t")
-                    kept["dy_t", grp, i // BANK_TOKENS] = dy_t
                 for u in range(2):
                     words = dy[:, u, i * WORDS : (i + 1) * WORDS, :].rearrange("p j e -> p (j e)").bitcast(F32)
-                    nc.tensor.transpose(dy_t[:, i % BANK_TOKENS, u, :], words, ident[:])
+                    nc.tensor.transpose(dy_t[:, i, u, :], words, ident[:])
 
         def interleave(grp):
             grouped = work.tile([P, SIZES[grp] * P * PACK], BF16, name="grouped", align_bytes=64)
             kept["grouped", grp] = grouped
-            for i in range(0, SIZES[grp], BANK_TOKENS):
-                T = min(BANK_TOKENS, SIZES[grp])
-                nc.scalar.copy(
-                    out=grouped[:, i * P * PACK : (i + T) * P * PACK].bitcast(F32).rearrange(
-                        "p (i t u) -> p i t u", i=T, u=2
-                    ),
-                    in_=kept["dy_t", grp, i // BANK_TOKENS][:].rearrange("p i u t -> p i t u"),
-                )
+            nc.scalar.copy(
+                out=grouped[:].bitcast(F32).rearrange("p (i t u) -> p i t u", i=SIZES[grp], u=2),
+                in_=kept["dy_t", grp][:].rearrange("p i u t -> p i t u"),
+            )
 
         def quantise(grp):
             codes = mx.tile([P, SIZES[grp] * P], U32, name="codes", align_bytes=64)
@@ -246,22 +238,18 @@ def tile_vdl_t_v_kernel(tc, x_in, w, b, y, grad_out, out):
             return tile_no >= (VECTOR_EVEN_FROM if tile_no % 2 == 0 else VECTOR_ODD_FROM)
 
         def empty(grp, i, h):
-            together = SIZES[grp] if grp < PAIRED_STORES else 1
-            key = ("result", grp, i // together)
-            if key not in kept:
-                kept[key] = outs.tile([P, together, IN_F], F32, name="result")
-                kept["left", key] = [together * HALVES]
-            result = kept[key]
+            tile_no = FIRST[grp] + i
+            store = ("result", grp, i) in kept
+            if not store:
+                kept["result", grp, i] = outs.tile([P, IN_F], F32, name="result")
+            result = kept["result", grp, i]
             acc = kept["acc", grp, i, h]
-            place = result[:, i % together, half(h)]
             if h == 0 and on_vector(grp, i):
-                nc.vector.tensor_copy(out=place, in_=acc[:])
+                nc.vector.tensor_copy(out=result[:, half(h)], in_=acc[:])
             else:
-                nc.scalar.copy(out=place, in_=acc[:])
-            kept["left", key][0] -= 1
-            if kept["left", key][0] == 0:
-                first = FIRST[grp] + i // together * together
-                nc.sync.dma_start(out=out_view[:, first : first + together, :], in_=result[:])
+                nc.scalar.copy(out=result[:, half(h)], in_=acc[:])
+            if store:
+                nc.sync.dma_start(out=out_view[:, tile_no, :], in_=result[:])
 
         def is_group(grp):
             return 0 <= grp < GROUPS

@@ -25,8 +25,7 @@ HALVES = IN_F // N_HALF
 TOK_PER_PART = TOKENS // P
 SIZES = (1, 2, 2, 2, 2, 2, 2, 1, 1, 1)
 GROUPS = len(SIZES)
-CHUNKS = (1, 1, 1, 2, 2, 3)
-W_BEHIND_Y = 1
+CHUNKS = (1, 1, 1, 1, 2, 2, 2)
 SQUARES_ON_SCALAR = 4
 VECTOR_EVEN_FROM = 6
 VECTOR_ODD_FROM = 15
@@ -57,28 +56,37 @@ def tile_vdl_t_v_kernel(tc, x_in, w, b, y, grad_out, out):
         def half(h):
             return slice(h * N_HALF, (h + 1) * N_HALF)
 
-        y_sb = []
-        g_sb = []
+        y_sb = {}
+        g_sb = {}
         w_raw = []
-        done = 0
-        for k, chunk in enumerate(CHUNKS):
-            T = sum(SIZES[done : done + chunk])
-            rows = slice(FIRST[done], FIRST[done] + T)
-            y_t = loads.tile([P, T, OUT_F], F32, name="y%d" % k)
-            nc.sync.dma_start(out=y_t[:], in_=y_view[:, rows, :])
-            if k == W_BEHIND_Y:
-                for h in range(HALVES):
-                    w_half = loads.tile([P, PACK, N_HALF], BF16, name="w%d" % h)
-                    for u in range(2):
-                        nc.sync.dma_start(out=w_half[:, 2 * u : 2 * u + 2, :], in_=w_view[:, u, :, half(h)])
-                    w_raw.append(w_half)
-            g_t = loads.tile([P, T, OUT_F], BF16, name="g%d" % k)
-            nc.sync.dma_start(out=g_t[:], in_=g_view[:, rows, :])
-            for grp in range(done, done + chunk):
-                own = slice(FIRST[grp] - FIRST[done], FIRST[grp] - FIRST[done] + SIZES[grp])
-                y_sb.append(y_t[:, own, :])
-                g_sb.append(g_t[:, own, :])
-            done += chunk
+
+        def load(which, k):
+            chunk = range(sum(CHUNKS[:k]), sum(CHUNKS[: k + 1]))
+            tokens = slice(FIRST[chunk.start], FIRST[chunk.start] + sum(SIZES[grp] for grp in chunk))
+            T = tokens.stop - tokens.start
+            if which == "y":
+                tile, view, parts = loads.tile([P, T, OUT_F], F32, name="y%d" % k), y_view, y_sb
+            else:
+                tile, view, parts = loads.tile([P, T, OUT_F], BF16, name="g%d" % k), g_view, g_sb
+            nc.sync.dma_start(out=tile[:], in_=view[:, tokens, :])
+            for grp in chunk:
+                own = slice(FIRST[grp] - tokens.start, FIRST[grp] - tokens.start + SIZES[grp])
+                parts[grp] = tile[:, own, :]
+
+        def load_w():
+            for h in range(HALVES):
+                w_half = loads.tile([P, PACK, N_HALF], BF16, name="w%d" % h)
+                for u in range(2):
+                    nc.sync.dma_start(out=w_half[:, 2 * u : 2 * u + 2, :], in_=w_view[:, u, :, half(h)])
+                w_raw.append(w_half)
+
+        load("y", 0)
+        for k in range(len(CHUNKS)):
+            if k + 1 < len(CHUNKS):
+                load("y", k + 1)
+            load("g", k)
+            if k == 0:
+                load_w()
 
         warm_in = consts.tile([P, 1], F32, name="warm_in")
         warm_out = consts.tile([P, 1], F32, name="warm_out")
@@ -304,12 +312,12 @@ def tile_vdl_t_v_kernel(tc, x_in, w, b, y, grad_out, out):
                     not_positive(r + 1)
                 if ahead and on_scalar(r + 1):
                     squares(r + 1)
-                if r == 0:
-                    group_w(1)
                 if behind and SIZES[r - 2] > 1 and not on_vector(r - 2, 1):
                     empty(r - 2, 1, 0)
                 if ahead:
                     sin_of(r + 1)
+                if r == 0:
+                    group_w(1)
                 if behind and SIZES[r - 2] > 1:
                     empty(r - 2, 1, 1)
                 if behind and on_vector(r - 2, 0):

@@ -22,7 +22,6 @@ IN_F = 1024
 WORDS = OUT_F // PACK
 N_HALF = 512
 HALVES = IN_F // N_HALF
-TOK_PER_PART = TOKENS // P
 SIZES = (1, 2, 2, 2, 2, 2, 2, 1, 1, 1)
 GROUPS = len(SIZES)
 CHUNKS = (1, 1, 1, 1, 2, 2, 2)
@@ -39,9 +38,6 @@ BYTES = TOKENS * OUT_F * 4 + TOKENS * OUT_F * 2 + OUT_F * IN_F * 2 + TOKENS * IN
 def tile_vdl_t_v_kernel(tc, x_in, w, b, y, grad_out, out):
     nc = tc.nc
     FIRST = [sum(SIZES[:grp]) for grp in range(GROUPS)]
-    y_view = y.rearrange("(q i) k -> q i k", i=TOK_PER_PART)
-    g_view = grad_out.rearrange("(q i) k -> q i k", i=TOK_PER_PART)
-    out_view = out.rearrange("(q i) n -> q i n", i=TOK_PER_PART)
     w_view = w.rearrange("(p e u) n -> p u e n", e=PAIR, u=2)
 
     with ExitStack() as ctx:
@@ -58,20 +54,26 @@ def tile_vdl_t_v_kernel(tc, x_in, w, b, y, grad_out, out):
 
         y_sb = {}
         g_sb = {}
+        out_rows = {}
         w_raw = []
+
+        def rows_of(tensor, tokens):
+            block = tensor[tokens.start * P : tokens.stop * P, :]
+            return block.rearrange("(q i) k -> q i k", i=tokens.stop - tokens.start)
 
         def load(which, k):
             chunk = range(sum(CHUNKS[:k]), sum(CHUNKS[: k + 1]))
             tokens = slice(FIRST[chunk.start], FIRST[chunk.start] + sum(SIZES[grp] for grp in chunk))
             T = tokens.stop - tokens.start
             if which == "y":
-                tile, view, parts = loads.tile([P, T, OUT_F], F32, name="y%d" % k), y_view, y_sb
+                tile, tensor, parts = loads.tile([P, T, OUT_F], F32, name="y%d" % k), y, y_sb
             else:
-                tile, view, parts = loads.tile([P, T, OUT_F], BF16, name="g%d" % k), g_view, g_sb
-            nc.sync.dma_start(out=tile[:], in_=view[:, tokens, :])
+                tile, tensor, parts = loads.tile([P, T, OUT_F], BF16, name="g%d" % k), grad_out, g_sb
+            nc.sync.dma_start(out=tile[:], in_=rows_of(tensor, tokens))
             for grp in chunk:
                 own = slice(FIRST[grp] - tokens.start, FIRST[grp] - tokens.start + SIZES[grp])
                 parts[grp] = tile[:, own, :]
+                out_rows[grp] = rows_of(out, tokens)[:, own, :]
 
         def load_w():
             for h in range(HALVES):
@@ -246,7 +248,6 @@ def tile_vdl_t_v_kernel(tc, x_in, w, b, y, grad_out, out):
             return tile_no >= (VECTOR_EVEN_FROM if tile_no % 2 == 0 else VECTOR_ODD_FROM)
 
         def empty(grp, i, h):
-            tile_no = FIRST[grp] + i
             store = ("result", grp, i) in kept
             if not store:
                 kept["result", grp, i] = outs.tile([P, IN_F], F32, name="result")
@@ -257,7 +258,7 @@ def tile_vdl_t_v_kernel(tc, x_in, w, b, y, grad_out, out):
             else:
                 nc.scalar.copy(out=result[:, half(h)], in_=acc[:])
             if store:
-                nc.sync.dma_start(out=out_view[:, tile_no, :], in_=result[:])
+                nc.sync.dma_start(out=out_rows[grp][:, i, :], in_=result[:])
 
         def is_group(grp):
             return 0 <= grp < GROUPS

@@ -26,8 +26,8 @@ SIZES = (1, 2, 2, 2, 2, 2, 2, 1, 1, 1)
 GROUPS = len(SIZES)
 CHUNKS = (1, 1, 1, 1, 2, 2, 2)
 SQUARES_ON_SCALAR = 4
-VECTOR_EVEN_FROM = 6
-VECTOR_ODD_FROM = 15
+VECTOR_EVEN_FROM = 8
+VECTOR_ODD_FROM = 13
 
 ROUND_MAGIC = 12582912.0
 

from contextlib import ExitStack
import math

import concourse.mybir as mybir
from concourse.masks import make_identity

F32 = mybir.dt.float32
BF16 = mybir.dt.bfloat16
U32 = mybir.dt.uint32
U8 = mybir.dt.uint8
E5M2X4 = mybir.dt.float8_e5m2_x4
E4M3X4 = mybir.dt.float8_e4m3fn_x4
ACT = mybir.ActivationFunctionType
ALU = mybir.AluOpType

P = 128
PACK = 4
PAIR = 2
TOKENS = 2048
OUT_F = 512
IN_F = 1024
WORDS = OUT_F // PACK
N_HALF = 512
HALVES = IN_F // N_HALF
SIZES = (1, 2, 2, 2, 2, 2, 2, 1, 1, 1)
GROUPS = len(SIZES)
CHUNKS = (1, 1, 1, 1, 2, 2, 2)
SQUARES_ON_SCALAR = 4
VECTOR_EVEN_FROM = 8
VECTOR_ODD_FROM = 13

ROUND_MAGIC = 12582912.0

FLOPS = 2 * TOKENS * OUT_F * IN_F
BYTES = TOKENS * OUT_F * 4 + TOKENS * OUT_F * 2 + OUT_F * IN_F * 2 + TOKENS * IN_F * 4


def tile_vdl_t_v_kernel(tc, x_in, w, b, y, grad_out, out):
    nc = tc.nc
    FIRST = [sum(SIZES[:grp]) for grp in range(GROUPS)]
    w_view = w.rearrange("(p e u) n -> p u e n", e=PAIR, u=2)

    with ExitStack() as ctx:
        consts = ctx.enter_context(tc.tile_pool(name="consts", bufs=1))
        loads = ctx.enter_context(tc.tile_pool(name="loads", bufs=1))
        work = ctx.enter_context(tc.tile_pool(name="work", bufs=3))
        mx = ctx.enter_context(tc.tile_pool(name="mx", bufs=4))
        outs = ctx.enter_context(tc.tile_pool(name="outs", bufs=8))
        psum_t = ctx.enter_context(tc.psum_pool(name="psum_t", bufs=2))
        psum_o = ctx.enter_context(tc.psum_pool(name="psum_o", bufs=6))

        def half(h):
            return slice(h * N_HALF, (h + 1) * N_HALF)

        y_sb = {}
        g_sb = {}
        out_rows = {}
        w_raw = []

        def rows_of(tensor, tokens):
            block = tensor[tokens.start * P : tokens.stop * P, :]
            return block.rearrange("(q i) k -> q i k", i=tokens.stop - tokens.start)

        def load(which, k):
            chunk = range(sum(CHUNKS[:k]), sum(CHUNKS[: k + 1]))
            tokens = slice(FIRST[chunk.start], FIRST[chunk.start] + sum(SIZES[grp] for grp in chunk))
            T = tokens.stop - tokens.start
            if which == "y":
                tile, tensor, parts = loads.tile([P, T, OUT_F], F32, name="y%d" % k), y, y_sb
            else:
                tile, tensor, parts = loads.tile([P, T, OUT_F], BF16, name="g%d" % k), grad_out, g_sb
            nc.sync.dma_start(out=tile[:], in_=rows_of(tensor, tokens))
            for grp in chunk:
                own = slice(FIRST[grp] - tokens.start, FIRST[grp] - tokens.start + SIZES[grp])
                parts[grp] = tile[:, own, :]
                out_rows[grp] = rows_of(out, tokens)[:, own, :]

        def load_w():
            for h in range(HALVES):
                w_half = loads.tile([P, PACK, N_HALF], BF16, name="w%d" % h)
                for u in range(2):
                    nc.sync.dma_start(out=w_half[:, 2 * u : 2 * u + 2, :], in_=w_view[:, u, :, half(h)])
                w_raw.append(w_half)

        load("y", 0)
        for k in range(len(CHUNKS)):
            if k + 1 < len(CHUNKS):
                load("y", k + 1)
            load("g", k)
            if k == 0:
                load_w()

        warm_in = consts.tile([P, 1], F32, name="warm_in")
        warm_out = consts.tile([P, 1], F32, name="warm_out")
        nc.vector.memset(warm_in[:], 0.0)
        nc.scalar.activation(out=warm_out[:], in_=warm_in[:], func=ACT.Silu)

        ident = consts.tile([P, P], F32, name="ident")
        make_identity(nc, ident[:])

        w_grouped = consts.tile([P, IN_F, PACK], BF16, name="w_grouped", align_bytes=64)
        w_codes = consts.tile([P, IN_F], U32, name="w_codes", align_bytes=64)
        w_scales = consts.tile([P, IN_F], U8, name="w_scales", align_bytes=64)

        def group_w(h):
            grouped = w_grouped[:, half(h), :].rearrange("p (c i) t -> p c t i", i=4)
            raw = w_raw[h][:].rearrange("p t (c i) -> p c t i", i=4)
            if h == 0:
                nc.vector.tensor_scalar(out=grouped, in0=raw, scalar1=-1.0, scalar2=None, op0=ALU.mult)
            else:
                nc.scalar.activation(out=grouped, in_=raw, func=ACT.Copy, scale=-1.0)

        def quantise_w(h):
            nc.vector.quantize_mx(
                out=w_codes[:, half(h)].bitcast(E4M3X4),
                scales=w_scales[:, half(h)],
                in_=w_grouped[:, half(h), :].rearrange("p n t -> p (n t)"),
            )

        kept = {}

        def y_column(grp, c):
            return y_sb[grp].rearrange("p i (j c) -> p i j c", c=PACK)[:, :, :, c]

        def g_pairs(grp, u):
            return g_sb[grp].rearrange("p i (j e u) -> p (i j) e u", e=PAIR, u=2)[:, :, :, u]

        def new(name, grp, lead=(), dtype=F32):
            kept[name, grp] = work.tile([P] + list(lead) + [SIZES[grp], WORDS], dtype, name=name)
            return kept[name, grp]

        def turns_of(grp):
            nc.vector.tensor_scalar(
                out=new("turns", grp)[:], in0=y_column(grp, 1),
                scalar1=1.0 / (2.0 * math.pi), scalar2=0.25, op0=ALU.mult, op1=ALU.add,
            )

        def whole_of(grp):
            nc.vector.tensor_scalar(
                out=new("whole", grp)[:], in0=kept["turns", grp][:], scalar1=ROUND_MAGIC,
                scalar2=ROUND_MAGIC, op0=ALU.add, op1=ALU.subtract,
            )

        def frac_of(grp):
            nc.vector.tensor_tensor(
                out=new("frac", grp)[:], in0=kept["turns", grp][:], in1=kept["whole", grp][:],
                op=ALU.subtract,
            )

        def compact(grp):
            pair = work.tile([P, SIZES[grp] * WORDS, PAIR], F32, name="pair")
            kept["pair", grp] = pair
            nc.vector.tensor_copy(
                out=pair[:], in_=y_sb[grp].rearrange("p i (j c) -> p (i j) c", c=PACK)[:, :, 0:PACK:3]
            )

        def tanh_of(grp):
            new("wave", grp, (2,))
            th = new("th", grp, (2,))
            pair = kept["pair", grp][:].rearrange("p (i j) e -> p i j e", i=SIZES[grp])
            nc.scalar.activation(out=th[:, 0], in_=pair[:, :, :, 1], func=ACT.Tanh, scale=0.5)
            nc.scalar.activation(out=th[:, 1], in_=pair[:, :, :, 0], func=ACT.Tanh)

        def sin_of(grp):
            nc.scalar.activation(
                out=kept["wave", grp][:, 0], in_=kept["frac", grp][:], func=ACT.Sin, scale=-2.0 * math.pi
            )

        def on_scalar(grp):
            return grp < SQUARES_ON_SCALAR

        def squares(grp):
            th = kept["th", grp]
            sq = kept["flat", grp][:, 0:2]
            if on_scalar(grp):
                nc.scalar.activation(out=sq, in_=th[:], func=ACT.Square)
            else:
                nc.vector.tensor_tensor(out=sq, in0=th[:], in1=th[:], op=ALU.mult)

        def not_positive(grp):
            new("flat", grp, (3,))
            nc.vector.tensor_scalar(
                out=kept["flat", grp][:, 2], in0=y_column(grp, 2), scalar1=0.0, scalar2=None, op0=ALU.is_le
            )

        def minus_sigmoid(grp):
            nc.vector.tensor_scalar(
                out=kept["wave", grp][:, 1], in0=kept["flat", grp][:, 0], scalar1=0.25, scalar2=-0.25,
                op0=ALU.mult, op1=ALU.add,
            )

        def tanh_and_relu(grp):
            dy = work.tile([P, 2, SIZES[grp] * WORDS, PAIR], BF16, name="dy")
            kept["dy", grp] = dy
            nc.vector.scalar_tensor_tensor(
                out=dy[:, 0], in0=kept["flat", grp][:, 1:3].rearrange("p e i j -> p (i j) e"), scalar=1.0,
                in1=g_pairs(grp, 0), op0=ALU.subtract, op1=ALU.mult,
            )

        def sin_and_sigmoid(grp):
            nc.vector.tensor_tensor(
                out=kept["dy", grp][:, 1], in0=kept["wave", grp][:].rearrange("p e i j -> p (i j) e"),
                in1=g_pairs(grp, 1), op=ALU.mult,
            )

        def transposes(grp):
            dy = kept["dy", grp]
            dy_t = psum_t.tile([P, SIZES[grp], 2, P], F32, name="dy_t")
            kept["dy_t", grp] = dy_t
            for i in range(SIZES[grp]):
                for u in range(2):
                    words = dy[:, u, i * WORDS : (i + 1) * WORDS, :].rearrange("p j e -> p (j e)").bitcast(F32)
                    nc.tensor.transpose(dy_t[:, i, u, :], words, ident[:])

        def interleave(grp):
            grouped = work.tile([P, SIZES[grp] * P * PACK], BF16, name="grouped", align_bytes=64)
            kept["grouped", grp] = grouped
            nc.scalar.copy(
                out=grouped[:].bitcast(F32).rearrange("p (i t u) -> p i t u", i=SIZES[grp], u=2),
                in_=kept["dy_t", grp][:].rearrange("p i u t -> p i t u"),
            )

        def quantise(grp):
            codes = mx.tile([P, SIZES[grp] * P], U32, name="codes", align_bytes=64)
            scales = mx.tile([P, SIZES[grp] * P], U8, name="scales", align_bytes=64)
            nc.vector.quantize_mx(out=codes[:].bitcast(E5M2X4), scales=scales[:], in_=kept["grouped", grp][:])
            kept["codes", grp] = (codes, scales)

        def multiply(grp):
            codes, scales = kept["codes", grp]
            for i in range(SIZES[grp]):
                toks = slice(i * P, (i + 1) * P)
                for h in range(HALVES):
                    acc = psum_o.tile([P, N_HALF], F32, name="acc")
                    kept["acc", grp, i, h] = acc
                    nc.tensor.matmul_mx(
                        out=acc[:],
                        lhsT=codes[:, toks].bitcast(E5M2X4),
                        lhsT_scale=scales[:, toks],
                        rhs=w_codes[:, half(h)].bitcast(E4M3X4),
                        rhs_scale=w_scales[:, half(h)],
                        start=True,
                        stop=True,
                    )

        def on_vector(grp, i):
            tile_no = FIRST[grp] + i
            return tile_no >= (VECTOR_EVEN_FROM if tile_no % 2 == 0 else VECTOR_ODD_FROM)

        def empty(grp, i, h):
            store = ("result", grp, i) in kept
            if not store:
                kept["result", grp, i] = outs.tile([P, IN_F], F32, name="result")
            result = kept["result", grp, i]
            acc = kept["acc", grp, i, h]
            if h == 0 and on_vector(grp, i):
                nc.vector.tensor_copy(out=result[:, half(h)], in_=acc[:])
            else:
                nc.scalar.copy(out=result[:, half(h)], in_=acc[:])
            if store:
                nc.sync.dma_start(out=out_rows[grp][:, i, :], in_=result[:])

        def is_group(grp):
            return 0 <= grp < GROUPS

        with tc.manual_schedule():
            turns_of(0)
            compact(0)
            whole_of(0)
            not_positive(0)
            frac_of(0)
            tanh_of(0)
            sin_of(0)
            if on_scalar(0):
                squares(0)
            for r in range(GROUPS + 2):
                ahead = is_group(r + 1)
                behind = is_group(r - 2)
                if is_group(r - 1):
                    interleave(r - 1)
                if is_group(r) and not on_scalar(r):
                    squares(r)
                if ahead:
                    compact(r + 1)
                if ahead:
                    tanh_of(r + 1)
                if behind and not on_vector(r - 2, 0):
                    empty(r - 2, 0, 0)
                if behind:
                    empty(r - 2, 0, 1)
                if ahead:
                    turns_of(r + 1)
                if is_group(r):
                    minus_sigmoid(r)
                if is_group(r):
                    tanh_and_relu(r)
                if ahead:
                    whole_of(r + 1)
                if is_group(r):
                    sin_and_sigmoid(r)
                    transposes(r)
                if ahead:
                    frac_of(r + 1)
                if r == 0:
                    group_w(0)
                    quantise_w(0)
                if r == 1:
                    quantise_w(1)
                if is_group(r - 1):
                    quantise(r - 1)
                    multiply(r - 1)
                if ahead:
                    not_positive(r + 1)
                if ahead and on_scalar(r + 1):
                    squares(r + 1)
                if behind and SIZES[r - 2] > 1 and not on_vector(r - 2, 1):
                    empty(r - 2, 1, 0)
                if ahead:
                    sin_of(r + 1)
                if r == 0:
                    group_w(1)
                if behind and SIZES[r - 2] > 1:
                    empty(r - 2, 1, 1)
                if behind and on_vector(r - 2, 0):
                    empty(r - 2, 0, 0)
                if behind and SIZES[r - 2] > 1 and on_vector(r - 2, 1):
                    empty(r - 2, 1, 0)
